import numpy as np
import ml_dtypes


def mxq(x, axis, fmt="e4m3"):
    dtype, down = {"e4m3": (ml_dtypes.float8_e4m3fn, 7), "e5m2": (ml_dtypes.float8_e5m2, 14)}[fmt]
    v = np.moveaxis(np.asarray(x, np.float32).astype(ml_dtypes.bfloat16).astype(np.float64), axis, -1)
    blocks = v.reshape(v.shape[:-1] + (-1, 32))
    amax = np.abs(blocks).max(-1, keepdims=True)
    byte = np.maximum(np.where(amax > 0, np.frexp(amax)[1] - 1 + 127, 0) - down, 1)
    scale = np.exp2(byte - 127.0)
    codes = (blocks / scale).astype(np.float32).astype(dtype).astype(np.float64)
    return np.moveaxis((codes * scale).reshape(v.shape), -1, axis)


WIDE = False


def mx_kscale(k):
    if not WIDE:
        return np.ones(k)
    levels = np.array([10, -10, 5, -5, 0])
    a = np.random.permutation(np.resize(levels, k // 512 * 4)).reshape(k // 512, 4)
    idx = np.arange(k)
    return np.exp2(a[idx // 512, idx % 128 // 32])


BF16 = ml_dtypes.bfloat16


def bf(x):
    return np.asarray(x, np.float32).astype(BF16)


def f64(x):
    return np.asarray(x).astype(np.float64)


E2M1 = np.array([0.0, 0.5, 1.0, 1.5, 2.0, 3.0, 4.0, 6.0, -0.0, -0.5, -1.0, -1.5, -2.0, -3.0, -4.0, -6.0])


def pack_weight(w, fmt):
    k, n = w.shape
    w = f64(bf(w)).reshape(k // 32, 32, n)
    amax = np.abs(w).max(1)
    if fmt == "e4m3":
        byte = np.frexp(amax)[1] - 1 + 127 - 7
    else:
        mant, ex = np.frexp(amax / 6.0)
        byte = np.where(mant > 0.5, ex, ex - 1) + 127
    byte = np.clip(np.where(amax > 0, byte, 1), 1, 254)
    scaled = (w * np.exp2(127.0 - byte)[:, None, :]).reshape(k, n).astype(np.float32)
    by_word = np.ascontiguousarray(scaled.reshape(k // 512, 128, 4, n).transpose(0, 1, 3, 2))
    if fmt == "e4m3":
        words = by_word.astype(ml_dtypes.float8_e4m3fn).view(np.uint8)
    else:
        c = by_word.astype(ml_dtypes.float4_e2m1fn).view(np.uint8) & 0xF
        words = c[..., 0::2] | (c[..., 1::2] << 4)
    return np.ascontiguousarray(words), np.ascontiguousarray(byte.astype(np.uint8).reshape(k // 512, 16, n))


def unpack_weight(words, scales, fmt):
    g, p, n, _ = words.shape
    if fmt == "e4m3":
        vals = np.ascontiguousarray(words).view(ml_dtypes.float8_e4m3fn).astype(np.float64)
    else:
        nib = np.empty((g, p, n, 4), np.uint8)
        nib[..., 0::2] = words & 0xF
        nib[..., 1::2] = words >> 4
        vals = E2M1[nib]
    vals = vals * np.repeat(np.exp2(scales.astype(np.float64) - 127.0), 8, axis=1)[..., None]
    return vals.transpose(0, 1, 3, 2).reshape(g * 512, n)

def pack4(w):
    words, scales = pack_weight(w, "e2m1")
    return words.reshape(words.shape[0], 128, -1), scales


def unpack4(words, scales):
    return unpack_weight(words.reshape(words.shape[0], 128, -1, 2), scales, "e2m1")


B, S, HID, H, HK, D = 2, 256, 2048, 16, 4, 128
EPS = 1e-6
PRE = 0.004


def rmsnorm(v, w):
    var = np.mean(v * v, axis=-1, keepdims=True)
    return w * (v * (1.0 / np.sqrt(var + EPS)))


def rope(v, cos, sin):
    c = cos[:, :, None, :]
    sn = sin[:, :, None, :]
    v1, v2 = np.split(v, 2, axis=-1)
    rot = np.concatenate([-v2, v1], axis=-1)
    return v * c + rot * sn


def setup_inputs():
    s = mx_kscale(HID)
    hidden_states = bf(np.random.standard_normal((B, S, HID)) * s)
    cos = bf(np.cos(np.random.standard_normal((B, S, D))))
    sin = bf(np.sin(np.random.standard_normal((B, S, D))))
    wq = np.random.standard_normal((H * D, HID)) * PRE / np.sqrt(HID) / s
    wk = np.random.standard_normal((HK * D, HID)) * PRE / np.sqrt(HID) / s
    q_norm_w = bf(1.0 + 0.1 * np.random.standard_normal(D))
    k_norm_w = bf(1.0 + 0.1 * np.random.standard_normal(D))
    wq_words, wq_scales = pack4(np.ascontiguousarray(wq.T))
    wk_words, wk_scales = pack4(np.ascontiguousarray(wk.T))
    return {
        "hidden_states": hidden_states,
        "cos": cos,
        "sin": sin,
        "Wq_query_words": wq_words,
        "Wq_query_scales": wq_scales,
        "Wk_words": wk_words,
        "Wk_scales": wk_scales,
        "q_norm_w": q_norm_w,
        "k_norm_w": k_norm_w,
    }


def reference(hidden_states, cos, sin, Wq_query_words, Wq_query_scales, Wk_words, Wk_scales, q_norm_w, k_norm_w):
    xq = mxq(f64(hidden_states), 2, "e4m3")
    q = (xq @ unpack4(Wq_query_words, Wq_query_scales)).reshape(B, S, H, D)
    k = (xq @ unpack4(Wk_words, Wk_scales)).reshape(B, S, HK, D)
    q = rmsnorm(q, f64(q_norm_w))
    k = rmsnorm(k, f64(k_norm_w))
    q = rope(q, f64(cos), f64(sin))
    k = rope(k, f64(cos), f64(sin))
    return q, k

@@ -1,0 +1,234 @@
+from contextlib import ExitStack
+
+import concourse.mybir as mybir
+from concourse.masks import make_identity
+
+F32 = mybir.dt.float32
+BF16 = mybir.dt.bfloat16
+I32 = mybir.dt.int32
+U32 = mybir.dt.uint32
+U8 = mybir.dt.uint8
+FP8X4 = mybir.dt.float8_e4m3fn_x4
+FP4X4 = mybir.dt.float4_e2m1fn_x4
+ALU = mybir.AluOpType
+ACT = mybir.ActivationFunctionType
+
+P = 128
+TOKENS = 512
+TOKEN_TILES = TOKENS // P
+HID = 2048
+K_PASS = 512
+PASSES = HID // K_PASS
+HEAD = 128
+HALF = HEAD // 2
+N_TILE = 512
+HEADS_PER_BANK = N_TILE // HEAD
+Q_FEATURES = 2048
+K_FEATURES = 512
+FEATURES = Q_FEATURES + K_FEATURES
+EPS = 1e-6
+
+FLOPS = 2 * TOKENS * HID * FEATURES
+
+
+def tile_qwen3nextattentionforengine_pa_kernel(
+    tc,
+    hidden_states,
+    cos,
+    sin,
+    Wq_query_words,
+    Wq_query_scales,
+    Wk_words,
+    Wk_scales,
+    q_norm_w,
+    k_norm_w,
+    out_0,
+    out_1,
+):
+    nc = tc.nc
+    x_rows = hidden_states.rearrange("b s k -> (b s) k")
+    q_rows = out_0.rearrange("b s h d -> (b s) (h d)")
+    k_rows = out_1.rearrange("b s h d -> (b s) (h d)")
+
+    with ExitStack() as ctx:
+        keep = ctx.enter_context(tc.tile_pool(name="keep", bufs=1))
+        stage = ctx.enter_context(tc.tile_pool(name="stage", bufs=2))
+        small = ctx.enter_context(tc.tile_pool(name="small", bufs=4))
+        work = ctx.enter_context(tc.tile_pool(name="work", bufs=4))
+        psum_x = ctx.enter_context(tc.psum_pool(name="psum_x", bufs=2))
+        psum_acc = ctx.enter_context(tc.psum_pool(name="psum_acc", bufs=6))
+
+        x_sb = [keep.tile([P, HID], BF16, name="x_sb%d" % m) for m in range(TOKEN_TILES)]
+        chunks = []
+        for n in range(Q_FEATURES // N_TILE):
+            chunks.append(("q", Wq_query_words, n, q_rows))
+        for n in range(K_FEATURES // N_TILE):
+            chunks.append(("k", Wk_words, n, k_rows))
+        w_words = [
+            keep.tile([P, PASSES, 2 * N_TILE], U8, name="w_words%d" % c, align_bytes=64)
+            for c in range(len(chunks))
+        ]
+        w_scales = keep.tile([P, PASSES, FEATURES], U8, name="w_scales", align_bytes=64)
+
+        def load_x(m):
+            nc.sync.dma_start(out=x_sb[m][:], in_=x_rows[m * P : (m + 1) * P, :])
+
+        def load_words(c):
+            words, n = chunks[c][1], chunks[c][2]
+            by_partition = words.bitcast(I32).rearrange("g p w -> p g w")
+            width = 2 * N_TILE // 4
+            nc.sync.dma_start(
+                out=w_words[c][:].bitcast(I32),
+                in_=by_partition[:, :, n * width : (n + 1) * width],
+            )
+
+        def load_scales(scales, first_column, columns):
+            by_row = scales.bitcast(I32).rearrange("g (Q r) w -> r Q g w", r=4)
+            for r in range(4):
+                nc.sync.dma_start(
+                    out=w_scales[r:P:32, :, first_column : first_column + columns].bitcast(I32),
+                    in_=by_row[r],
+                )
+
+        nc.vector.memset(w_scales[:].bitcast(I32), 0)
+
+        load_x(0)
+        load_words(0)
+        cos_sb = keep.tile([P, TOKEN_TILES, HEAD], BF16, name="cos_sb")
+        sin_sb = keep.tile([P, TOKEN_TILES, HEAD], BF16, name="sin_sb")
+        nc.scalar.dma_start(out=cos_sb[:], in_=cos.rearrange("b (n p) d -> p (b n) d", p=P))
+        nc.scalar.dma_start(out=sin_sb[:], in_=sin.rearrange("b (n p) d -> p (b n) d", p=P))
+        gain = {}
+        for kind, vector in (("q", q_norm_w), ("k", k_norm_w)):
+            gain[kind] = keep.tile([P, HEAD], BF16, name="gain_" + kind)
+            nc.scalar.dma_start(out=gain[kind][:], in_=vector.partition_broadcast(P))
+        load_scales(Wq_query_scales, 0, Q_FEATURES)
+        for m in range(1, TOKEN_TILES):
+            load_x(m)
+        load_words(1)
+        load_scales(Wk_scales, Q_FEATURES, K_FEATURES)
+        for c in range(2, len(chunks)):
+            load_words(c)
+
+        ident = keep.tile([P, P], F32, name="ident")
+        make_identity(nc, ident[:])
+        eps = keep.tile([P, 1], F32, name="eps")
+        nc.vector.memset(eps[:], EPS)
+        warm = keep.tile([P, 1], F32, name="warm")
+        nc.scalar.activation(out=warm[:], in_=eps[:], func=ACT.Sqrt)
+
+        cos_w = {}
+        sin_w = {}
+        for kind in ("q", "k"):
+            w = gain[kind]
+            cos_w[kind] = keep.tile([P, TOKEN_TILES, HEAD], F32, name="cos_w_" + kind)
+            sin_w[kind] = keep.tile([P, TOKEN_TILES, HEAD], F32, name="sin_w_" + kind)
+            nc.vector.tensor_tensor(
+                out=cos_w[kind][:],
+                in0=cos_sb[:],
+                in1=w[:].unsqueeze(1).to_broadcast([P, TOKEN_TILES, HEAD]),
+                op=ALU.mult,
+            )
+            nc.vector.scalar_tensor_tensor(
+                out=sin_w[kind][:, :, 0:HALF],
+                in0=sin_sb[:, :, 0:HALF],
+                scalar=-1.0,
+                in1=w[:, HALF:HEAD].unsqueeze(1).to_broadcast([P, TOKEN_TILES, HALF]),
+                op0=ALU.mult,
+                op1=ALU.mult,
+            )
+            nc.vector.tensor_tensor(
+                out=sin_w[kind][:, :, HALF:HEAD],
+                in0=sin_sb[:, :, HALF:HEAD],
+                in1=w[:, 0:HALF].unsqueeze(1).to_broadcast([P, TOKEN_TILES, HALF]),
+                op=ALU.mult,
+            )
+
+        x_codes = [keep.tile([P, PASSES * P], U32, name="x_codes%d" % m, align_bytes=64) for m in range(TOKEN_TILES)]
+        x_scales = [keep.tile([P, PASSES * P], U8, name="x_scales%d" % m, align_bytes=64) for m in range(TOKEN_TILES)]
+
+        def quantise_tokens(m):
+            words = x_sb[m][:].bitcast(F32)
+            grouped = stage.tile([P, PASSES * P * 4], BF16, name="grouped", align_bytes=64)
+            grouped_words = grouped[:].bitcast(F32).rearrange("p (g t u) -> p g t u", g=PASSES, u=2)
+            for pair in range(PASSES // 2):
+                flipped = psum_x.tile([P, 2, 2, P], F32, name="flipped")
+                for i in range(2):
+                    g = 2 * pair + i
+                    for u in range(2):
+                        nc.tensor.transpose(
+                            flipped[:, i, u, :],
+                            words[:, 256 * g + u : 256 * (g + 1) : 2],
+                            ident[:],
+                        )
+                nc.scalar.copy(
+                    out=grouped_words[:, 2 * pair : 2 * pair + 2, :, :],
+                    in_=flipped[:].rearrange("p i u t -> p i t u"),
+                )
+            nc.vector.quantize_mx(
+                out=x_codes[m][:].bitcast(FP8X4), scales=x_scales[m][:], in_=grouped[:]
+            )
+
+        squares = keep.tile([P, HEAD], F32, name="squares")
+
+        def project(c, m):
+            acc = psum_acc.tile([P, N_TILE], F32, name="acc")
+            for g in range(PASSES):
+                nc.tensor.matmul_mx(
+                    out=acc[:],
+                    lhsT=x_codes[m][:, g * P : (g + 1) * P].bitcast(FP8X4),
+                    lhsT_scale=x_scales[m][:, g * P : (g + 1) * P],
+                    rhs=w_words[c][:, g, :].bitcast(FP4X4),
+                    rhs_scale=w_scales[:, g, c * N_TILE : (c + 1) * N_TILE],
+                    start=(g == 0),
+                    stop=(g == PASSES - 1),
+                )
+            return acc
+
+        def norm_and_rotate(c, m, acc):
+            kind, n, rows = chunks[c][0], chunks[c][2], chunks[c][3]
+            sum_sq = small.tile([P, HEADS_PER_BANK], F32, name="sum_sq")
+            for h in range(HEADS_PER_BANK):
+                nc.scalar.activation(
+                    out=squares[:],
+                    in_=acc[:, h * HEAD : (h + 1) * HEAD],
+                    func=ACT.Square,
+                    accum_out=sum_sq[:, h : h + 1],
+                )
+            std = small.tile([P, HEADS_PER_BANK], F32, name="std")
+            nc.scalar.activation(out=std[:], in_=sum_sq[:], func=ACT.Sqrt, scale=1.0 / HEAD, bias=eps[:, 0:1])
+            rstd = small.tile([P, HEADS_PER_BANK], F32, name="rstd")
+            nc.vector.reciprocal(out=rstd[:], in_=std[:])
+
+            straight = work.tile([P, N_TILE], F32, name="straight")
+            crossed = work.tile([P, N_TILE], F32, name="crossed")
+            for h in range(HEADS_PER_BANK):
+                first = h * HEAD
+                nc.vector.scalar_tensor_tensor(
+                    out=straight[:, first : first + HEAD],
+                    in0=acc[:, first : first + HEAD],
+                    scalar=rstd[:, h : h + 1],
+                    in1=cos_w[kind][:, m, :],
+                    op0=ALU.mult,
+                    op1=ALU.mult,
+                )
+                for here, there in ((0, HALF), (HALF, 0)):
+                    nc.vector.scalar_tensor_tensor(
+                        out=crossed[:, first + here : first + here + HALF],
+                        in0=acc[:, first + there : first + there + HALF],
+                        scalar=rstd[:, h : h + 1],
+                        in1=sin_w[kind][:, m, here : here + HALF],
+                        op0=ALU.mult,
+                        op1=ALU.mult,
+                    )
+            result = work.tile([P, N_TILE], F32, name="result")
+            nc.gpsimd.tensor_tensor(out=result[:], in0=straight[:], in1=crossed[:], op=ALU.add)
+            nc.sync.dma_start(
+                out=rows[m * P : (m + 1) * P, n * N_TILE : (n + 1) * N_TILE], in_=result[:]
+            )
+
+        for c in range(len(chunks)):
+            for m in range(TOKEN_TILES):
+                if c == 0:
+                    quantise_tokens(m)
+                norm_and_rotate(c, m, project(c, m))

@@ -27,6 +27,9 @@ Q_FEATURES = 2048
 K_FEATURES = 512
 FEATURES = Q_FEATURES + K_FEATURES
 EPS = 1e-6
+PROJECT_AHEAD = 4
+ROTATE_AHEAD = 2
+PREPARE_AHEAD = 2
 
 FLOPS = 2 * TOKENS * HID * FEATURES
 
@@ -53,8 +56,9 @@ def tile_qwen3nextattentionforengine_pa_kernel(
     with ExitStack() as ctx:
         keep = ctx.enter_context(tc.tile_pool(name="keep", bufs=1))
         stage = ctx.enter_context(tc.tile_pool(name="stage", bufs=2))
-        small = ctx.enter_context(tc.tile_pool(name="small", bufs=4))
-        work = ctx.enter_context(tc.tile_pool(name="work", bufs=4))
+        small = ctx.enter_context(tc.tile_pool(name="small", bufs=8))
+        products = ctx.enter_context(tc.tile_pool(name="products", bufs=3))
+        results = ctx.enter_context(tc.tile_pool(name="results", bufs=6))
         psum_x = ctx.enter_context(tc.psum_pool(name="psum_x", bufs=2))
         psum_acc = ctx.enter_context(tc.psum_pool(name="psum_acc", bufs=6))
 
@@ -90,39 +94,32 @@ def tile_qwen3nextattentionforengine_pa_kernel(
                     in_=by_row[r],
                 )
 
-        nc.vector.memset(w_scales[:].bitcast(I32), 0)
-
-        load_x(0)
-        load_words(0)
         cos_sb = keep.tile([P, TOKEN_TILES, HEAD], BF16, name="cos_sb")
         sin_sb = keep.tile([P, TOKEN_TILES, HEAD], BF16, name="sin_sb")
-        nc.scalar.dma_start(out=cos_sb[:], in_=cos.rearrange("b (n p) d -> p (b n) d", p=P))
-        nc.scalar.dma_start(out=sin_sb[:], in_=sin.rearrange("b (n p) d -> p (b n) d", p=P))
-        gain = {}
-        for kind, vector in (("q", q_norm_w), ("k", k_norm_w)):
-            gain[kind] = keep.tile([P, HEAD], BF16, name="gain_" + kind)
-            nc.scalar.dma_start(out=gain[kind][:], in_=vector.partition_broadcast(P))
-        load_scales(Wq_query_scales, 0, Q_FEATURES)
-        for m in range(1, TOKEN_TILES):
-            load_x(m)
-        load_words(1)
-        load_scales(Wk_scales, Q_FEATURES, K_FEATURES)
-        for c in range(2, len(chunks)):
-            load_words(c)
-
+        gain = {
+            "q": keep.tile([P, HEAD], BF16, name="gain_q"),
+            "k": keep.tile([P, HEAD], BF16, name="gain_k"),
+        }
         ident = keep.tile([P, P], F32, name="ident")
-        make_identity(nc, ident[:])
         eps = keep.tile([P, 1], F32, name="eps")
-        nc.vector.memset(eps[:], EPS)
         warm = keep.tile([P, 1], F32, name="warm")
-        nc.scalar.activation(out=warm[:], in_=eps[:], func=ACT.Sqrt)
-
         cos_w = {}
         sin_w = {}
         for kind in ("q", "k"):
-            w = gain[kind]
             cos_w[kind] = keep.tile([P, TOKEN_TILES, HEAD], F32, name="cos_w_" + kind)
             sin_w[kind] = keep.tile([P, TOKEN_TILES, HEAD], F32, name="sin_w_" + kind)
+        x_codes = [
+            keep.tile([P, PASSES * P], U32, name="x_codes%d" % m, align_bytes=64)
+            for m in range(TOKEN_TILES)
+        ]
+        x_scales = [
+            keep.tile([P, PASSES * P], U8, name="x_scales%d" % m, align_bytes=64)
+            for m in range(TOKEN_TILES)
+        ]
+        squares = keep.tile([P, HEADS_PER_BANK, HEAD], F32, name="squares")
+
+        def build_tables(kind):
+            w = gain[kind]
             nc.vector.tensor_tensor(
                 out=cos_w[kind][:],
                 in0=cos_sb[:],
@@ -144,10 +141,7 @@ def tile_qwen3nextattentionforengine_pa_kernel(
                 op=ALU.mult,
             )
 
-        x_codes = [keep.tile([P, PASSES * P], U32, name="x_codes%d" % m, align_bytes=64) for m in range(TOKEN_TILES)]
-        x_scales = [keep.tile([P, PASSES * P], U8, name="x_scales%d" % m, align_bytes=64) for m in range(TOKEN_TILES)]
-
-        def quantise_tokens(m):
+        def prepare_tokens(m):
             words = x_sb[m][:].bitcast(F32)
             grouped = stage.tile([P, PASSES * P * 4], BF16, name="grouped", align_bytes=64)
             grouped_words = grouped[:].bitcast(F32).rearrange("p (g t u) -> p g t u", g=PASSES, u=2)
@@ -161,7 +155,8 @@ def tile_qwen3nextattentionforengine_pa_kernel(
                             words[:, 256 * g + u : 256 * (g + 1) : 2],
                             ident[:],
                         )
-                nc.scalar.copy(
+                copy = nc.scalar.copy if pair == 0 else nc.vector.tensor_copy
+                copy(
                     out=grouped_words[:, 2 * pair : 2 * pair + 2, :, :],
                     in_=flipped[:].rearrange("p i u t -> p i t u"),
                 )
@@ -169,13 +164,11 @@ def tile_qwen3nextattentionforengine_pa_kernel(
                 out=x_codes[m][:].bitcast(FP8X4), scales=x_scales[m][:], in_=grouped[:]
             )
 
-        squares = keep.tile([P, HEAD], F32, name="squares")
-
-        def project(c, m):
-            acc = psum_acc.tile([P, N_TILE], F32, name="acc")
+        def project(m, c):
+            acc = psum_acc.tile([P, HEADS_PER_BANK, HEAD], F32, name="acc")
             for g in range(PASSES):
                 nc.tensor.matmul_mx(
-                    out=acc[:],
+                    out=acc[:].rearrange("p h d -> p (h d)"),
                     lhsT=x_codes[m][:, g * P : (g + 1) * P].bitcast(FP8X4),
                     lhsT_scale=x_scales[m][:, g * P : (g + 1) * P],
                     rhs=w_words[c][:, g, :].bitcast(FP4X4),
@@ -185,50 +178,99 @@ def tile_qwen3nextattentionforengine_pa_kernel(
                 )
             return acc
 
-        def norm_and_rotate(c, m, acc):
-            kind, n, rows = chunks[c][0], chunks[c][2], chunks[c][3]
+        def sum_squares(acc):
             sum_sq = small.tile([P, HEADS_PER_BANK], F32, name="sum_sq")
             for h in range(HEADS_PER_BANK):
                 nc.scalar.activation(
-                    out=squares[:],
-                    in_=acc[:, h * HEAD : (h + 1) * HEAD],
-                    func=ACT.Square,
-                    accum_out=sum_sq[:, h : h + 1],
+                    out=squares[:, h, :], in_=acc[:, h, :], func=ACT.Square, accum_out=sum_sq[:, h : h + 1]
                 )
-            std = small.tile([P, HEADS_PER_BANK], F32, name="std")
-            nc.scalar.activation(out=std[:], in_=sum_sq[:], func=ACT.Sqrt, scale=1.0 / HEAD, bias=eps[:, 0:1])
-            rstd = small.tile([P, HEADS_PER_BANK], F32, name="rstd")
-            nc.vector.reciprocal(out=rstd[:], in_=std[:])
+            return sum_sq
 
-            straight = work.tile([P, N_TILE], F32, name="straight")
-            crossed = work.tile([P, N_TILE], F32, name="crossed")
-            for h in range(HEADS_PER_BANK):
-                first = h * HEAD
-                nc.vector.scalar_tensor_tensor(
-                    out=straight[:, first : first + HEAD],
-                    in0=acc[:, first : first + HEAD],
-                    scalar=rstd[:, h : h + 1],
-                    in1=cos_w[kind][:, m, :],
-                    op0=ALU.mult,
-                    op1=ALU.mult,
+        def inverse_rms(sum_sq):
+            rstd = small.tile([P, HEADS_PER_BANK], F32, name="rstd")
+            nc.scalar.activation(
+                out=rstd[:], in_=sum_sq[:], func=ACT.Abs_reciprocal_sqrt, scale=1.0 / HEAD, bias=eps[:, 0:1]
+            )
+            return rstd
+
+        def rotate(m, c, acc):
+            kind = chunks[c][0]
+            straight = products.tile([P, HEADS_PER_BANK, HEAD], F32, name="straight")
+            crossed = products.tile([P, HEADS_PER_BANK, HEAD], F32, name="crossed")
+            nc.vector.tensor_tensor(
+                out=straight[:],
+                in0=acc[:],
+                in1=cos_w[kind][:, m, :].unsqueeze(1).to_broadcast([P, HEADS_PER_BANK, HEAD]),
+                op=ALU.mult,
+            )
+            for here, there in ((0, HALF), (HALF, 0)):
+                nc.vector.tensor_tensor(
+                    out=crossed[:, :, here : here + HALF],
+                    in0=acc[:, :, there : there + HALF],
+                    in1=sin_w[kind][:, m, here : here + HALF]
+                    .unsqueeze(1)
+                    .to_broadcast([P, HEADS_PER_BANK, HALF]),
+                    op=ALU.mult,
                 )
-                for here, there in ((0, HALF), (HALF, 0)):
-                    nc.vector.scalar_tensor_tensor(
-                        out=crossed[:, first + here : first + here + HALF],
-                        in0=acc[:, first + there : first + there + HALF],
-                        scalar=rstd[:, h : h + 1],
-                        in1=sin_w[kind][:, m, here : here + HALF],
-                        op0=ALU.mult,
-                        op1=ALU.mult,
-                    )
-            result = work.tile([P, N_TILE], F32, name="result")
-            nc.gpsimd.tensor_tensor(out=result[:], in0=straight[:], in1=crossed[:], op=ALU.add)
+            rotated = results.tile([P, HEADS_PER_BANK, HEAD], F32, name="rotated")
+            nc.gpsimd.tensor_tensor(out=rotated[:], in0=straight[:], in1=crossed[:], op=ALU.add)
+            return rotated
+
+        def scale_and_store(m, c, rotated, rstd):
+            n, rows = chunks[c][2], chunks[c][3]
+            for h in range(HEADS_PER_BANK):
+                nc.scalar.activation(
+                    out=rotated[:, h, :], in_=rotated[:, h, :], func=ACT.Copy, scale=rstd[:, h : h + 1]
+                )
             nc.sync.dma_start(
-                out=rows[m * P : (m + 1) * P, n * N_TILE : (n + 1) * N_TILE], in_=result[:]
+                out=rows[m * P : (m + 1) * P, n * N_TILE : (n + 1) * N_TILE],
+                in_=rotated[:].rearrange("p h d -> p (h d)"),
             )
 
-        for c in range(len(chunks)):
-            for m in range(TOKEN_TILES):
-                if c == 0:
-                    quantise_tokens(m)
-                norm_and_rotate(c, m, project(c, m))
+        ctx.enter_context(tc.manual_schedule())
+
+        nc.vector.memset(w_scales[:].bitcast(I32), 0)
+        nc.vector.memset(eps[:], EPS)
+        make_identity(nc, ident[:])
+
+        load_x(0)
+        load_words(0)
+        nc.scalar.dma_start(out=cos_sb[:], in_=cos.rearrange("b (n p) d -> p (b n) d", p=P))
+        nc.scalar.dma_start(out=sin_sb[:], in_=sin.rearrange("b (n p) d -> p (b n) d", p=P))
+        nc.gpsimd.dma_start(out=gain["q"][:], in_=q_norm_w.partition_broadcast(P))
+        nc.gpsimd.dma_start(out=gain["k"][:], in_=k_norm_w.partition_broadcast(P))
+        load_scales(Wq_query_scales, 0, Q_FEATURES)
+        load_words(1)
+        load_words(2)
+        load_scales(Wk_scales, Q_FEATURES, K_FEATURES)
+        load_words(3)
+        load_words(4)
+        for m in range(1, TOKEN_TILES):
+            load_x(m)
+
+        nc.scalar.activation(out=warm[:], in_=eps[:], func=ACT.Abs_reciprocal_sqrt)
+
+        banks = [(m, c) for m in range(TOKEN_TILES) for c in range(len(chunks))]
+        acc = {}
+        sum_sq = {}
+        rstd = {}
+        rotated = {}
+
+        prepare_tokens(0)
+        build_tables("q")
+        build_tables("k")
+        for last in range(-PROJECT_AHEAD, len(banks)):
+            first = last + PROJECT_AHEAD
+            middle = last + ROTATE_AHEAD
+            if first < len(banks):
+                soon = first + PREPARE_AHEAD
+                if soon % len(chunks) == 0 and soon < len(banks):
+                    prepare_tokens(soon // len(chunks))
+                acc[first] = project(banks[first][0], banks[first][1])
+                sum_sq[first] = sum_squares(acc[first])
+            if 0 <= middle < len(banks):
+                rotated[middle] = rotate(banks[middle][0], banks[middle][1], acc[middle])
+            if last >= 0:
+                scale_and_store(banks[last][0], banks[last][1], rotated[last], rstd[last])
+            if first < len(banks):
+                rstd[first] = inverse_rms(sum_sq[first])

@@ -28,7 +28,8 @@ K_FEATURES = 512
 FEATURES = Q_FEATURES + K_FEATURES
 EPS = 1e-6
 PROJECT_AHEAD = 4
-ROTATE_AHEAD = 2
+MULTIPLY_AHEAD = 2
+ADD_AHEAD = 1
 PREPARE_AHEAD = 2
 
 FLOPS = 2 * TOKENS * HID * FEATURES
@@ -193,9 +194,9 @@ def tile_qwen3nextattentionforengine_pa_kernel(
             )
             return rstd
 
-        def rotate(m, c, acc):
+        def multiply(m, c, acc):
             kind = chunks[c][0]
-            straight = products.tile([P, HEADS_PER_BANK, HEAD], F32, name="straight")
+            straight = results.tile([P, HEADS_PER_BANK, HEAD], F32, name="straight")
             crossed = products.tile([P, HEADS_PER_BANK, HEAD], F32, name="crossed")
             nc.vector.tensor_tensor(
                 out=straight[:],
@@ -212,9 +213,10 @@ def tile_qwen3nextattentionforengine_pa_kernel(
                     .to_broadcast([P, HEADS_PER_BANK, HALF]),
                     op=ALU.mult,
                 )
-            rotated = results.tile([P, HEADS_PER_BANK, HEAD], F32, name="rotated")
-            nc.gpsimd.tensor_tensor(out=rotated[:], in0=straight[:], in1=crossed[:], op=ALU.add)
-            return rotated
+            return straight, crossed
+
+        def add(straight, crossed):
+            nc.vector.tensor_tensor(out=straight[:], in0=straight[:], in1=crossed[:], op=ALU.add)
 
         def scale_and_store(m, c, rotated, rstd):
             n, rows = chunks[c][2], chunks[c][3]
@@ -242,11 +244,12 @@ def tile_qwen3nextattentionforengine_pa_kernel(
         load_scales(Wq_query_scales, 0, Q_FEATURES)
         load_words(1)
         load_words(2)
-        load_scales(Wk_scales, Q_FEATURES, K_FEATURES)
         load_words(3)
+        load_x(1)
+        load_scales(Wk_scales, Q_FEATURES, K_FEATURES)
         load_words(4)
-        for m in range(1, TOKEN_TILES):
-            load_x(m)
+        load_x(2)
+        load_x(3)
 
         nc.scalar.activation(out=warm[:], in_=eps[:], func=ACT.Abs_reciprocal_sqrt)
 
@@ -254,23 +257,27 @@ def tile_qwen3nextattentionforengine_pa_kernel(
         acc = {}
         sum_sq = {}
         rstd = {}
-        rotated = {}
+        straight = {}
+        crossed = {}
 
         prepare_tokens(0)
         build_tables("q")
         build_tables("k")
         for last in range(-PROJECT_AHEAD, len(banks)):
             first = last + PROJECT_AHEAD
-            middle = last + ROTATE_AHEAD
+            second = last + MULTIPLY_AHEAD
+            third = last + ADD_AHEAD
             if first < len(banks):
                 soon = first + PREPARE_AHEAD
                 if soon % len(chunks) == 0 and soon < len(banks):
                     prepare_tokens(soon // len(chunks))
                 acc[first] = project(banks[first][0], banks[first][1])
                 sum_sq[first] = sum_squares(acc[first])
-            if 0 <= middle < len(banks):
-                rotated[middle] = rotate(banks[middle][0], banks[middle][1], acc[middle])
+            if 0 <= second < len(banks):
+                straight[second], crossed[second] = multiply(banks[second][0], banks[second][1], acc[second])
+            if 0 <= third < len(banks):
+                add(straight[third], crossed[third])
             if last >= 0:
-                scale_and_store(banks[last][0], banks[last][1], rotated[last], rstd[last])
+                scale_and_store(banks[last][0], banks[last][1], straight[last], rstd[last])
             if first < len(banks):
                 rstd[first] = inverse_rms(sum_sq[first])

@@ -28,8 +28,7 @@ K_FEATURES = 512
 FEATURES = Q_FEATURES + K_FEATURES
 EPS = 1e-6
 PROJECT_AHEAD = 4
-MULTIPLY_AHEAD = 2
-ADD_AHEAD = 1
+ROTATE_AHEAD = 2
 PREPARE_AHEAD = 2
 
 FLOPS = 2 * TOKENS * HID * FEATURES
@@ -50,9 +49,11 @@ def tile_qwen3nextattentionforengine_pa_kernel(
     out_1,
 ):
     nc = tc.nc
-    x_rows = hidden_states.rearrange("b s k -> (b s) k")
-    q_rows = out_0.rearrange("b s h d -> (b s) (h d)")
-    k_rows = out_1.rearrange("b s h d -> (b s) (h d)")
+    x_tiles = hidden_states.rearrange("b s k -> (b s) k").rearrange("(p m) k -> m p k", m=TOKEN_TILES)
+    q_tiles = out_0.rearrange("b s h d -> (b s) (h d)").rearrange("(p m) f -> m p f", m=TOKEN_TILES)
+    k_tiles = out_1.rearrange("b s h d -> (b s) (h d)").rearrange("(p m) f -> m p f", m=TOKEN_TILES)
+    cos_tiles = cos.rearrange("b s d -> (b s) d").rearrange("(p m) d -> p m d", m=TOKEN_TILES)
+    sin_tiles = sin.rearrange("b s d -> (b s) d").rearrange("(p m) d -> p m d", m=TOKEN_TILES)
 
     with ExitStack() as ctx:
         keep = ctx.enter_context(tc.tile_pool(name="keep", bufs=1))
@@ -66,20 +67,30 @@ def tile_qwen3nextattentionforengine_pa_kernel(
         x_sb = [keep.tile([P, HID], BF16, name="x_sb%d" % m) for m in range(TOKEN_TILES)]
         chunks = []
         for n in range(Q_FEATURES // N_TILE):
-            chunks.append(("q", Wq_query_words, n, q_rows))
+            chunks.append(("q", Wq_query_words, Wq_query_scales, n, q_tiles))
         for n in range(K_FEATURES // N_TILE):
-            chunks.append(("k", Wk_words, n, k_rows))
+            chunks.append(("k", Wk_words, Wk_scales, n, k_tiles))
         w_words = [
             keep.tile([P, PASSES, 2 * N_TILE], U8, name="w_words%d" % c, align_bytes=64)
             for c in range(len(chunks))
         ]
-        w_scales = keep.tile([P, PASSES, FEATURES], U8, name="w_scales", align_bytes=64)
+        w_scales = [
+            keep.tile([P, PASSES, N_TILE], U8, name="w_scales%d" % c, align_bytes=64)
+            for c in range(len(chunks))
+        ]
 
         def load_x(m):
-            nc.sync.dma_start(out=x_sb[m][:], in_=x_rows[m * P : (m + 1) * P, :])
+            nc.sync.dma_start(out=x_sb[m][:], in_=x_tiles[m])
 
-        def load_words(c):
-            words, n = chunks[c][1], chunks[c][2]
+        def load_chunk(c):
+            words, scales, n = chunks[c][1], chunks[c][2], chunks[c][3]
+            by_row = scales.bitcast(I32).rearrange("g (Q r) w -> r Q g w", r=4)
+            width = N_TILE // 4
+            for r in range(4):
+                nc.sync.dma_start(
+                    out=w_scales[c][r:P:32, :, :].bitcast(I32),
+                    in_=by_row[r][:, :, n * width : (n + 1) * width],
+                )
             by_partition = words.bitcast(I32).rearrange("g p w -> p g w")
             width = 2 * N_TILE // 4
             nc.sync.dma_start(
@@ -87,20 +98,10 @@ def tile_qwen3nextattentionforengine_pa_kernel(
                 in_=by_partition[:, :, n * width : (n + 1) * width],
             )
 
-        def load_scales(scales, first_column, columns):
-            by_row = scales.bitcast(I32).rearrange("g (Q r) w -> r Q g w", r=4)
-            for r in range(4):
-                nc.sync.dma_start(
-                    out=w_scales[r:P:32, :, first_column : first_column + columns].bitcast(I32),
-                    in_=by_row[r],
-                )
-
         cos_sb = keep.tile([P, TOKEN_TILES, HEAD], BF16, name="cos_sb")
         sin_sb = keep.tile([P, TOKEN_TILES, HEAD], BF16, name="sin_sb")
-        gain = {
-            "q": keep.tile([P, HEAD], BF16, name="gain_q"),
-            "k": keep.tile([P, HEAD], BF16, name="gain_k"),
-        }
+        ones = keep.tile([P, P], BF16, name="ones")
+        gain_rows = keep.tile([P, 2, HEAD], BF16, name="gain_rows")
         ident = keep.tile([P, P], F32, name="ident")
         eps = keep.tile([P, 1], F32, name="eps")
         warm = keep.tile([P, 1], F32, name="warm")
@@ -119,12 +120,11 @@ def tile_qwen3nextattentionforengine_pa_kernel(
         ]
         squares = keep.tile([P, HEADS_PER_BANK, HEAD], F32, name="squares")
 
-        def build_tables(kind):
-            w = gain[kind]
+        def build_tables(kind, w):
             nc.vector.tensor_tensor(
                 out=cos_w[kind][:],
                 in0=cos_sb[:],
-                in1=w[:].unsqueeze(1).to_broadcast([P, TOKEN_TILES, HEAD]),
+                in1=w.unsqueeze(1).to_broadcast([P, TOKEN_TILES, HEAD]),
                 op=ALU.mult,
             )
             nc.vector.scalar_tensor_tensor(
@@ -146,24 +146,29 @@ def tile_qwen3nextattentionforengine_pa_kernel(
             words = x_sb[m][:].bitcast(F32)
             grouped = stage.tile([P, PASSES * P * 4], BF16, name="grouped", align_bytes=64)
             grouped_words = grouped[:].bitcast(F32).rearrange("p (g t u) -> p g t u", g=PASSES, u=2)
+            flipped = []
             for pair in range(PASSES // 2):
-                flipped = psum_x.tile([P, 2, 2, P], F32, name="flipped")
+                flipped.append(psum_x.tile([P, 2, 2, P], F32, name="flipped"))
                 for i in range(2):
                     g = 2 * pair + i
                     for u in range(2):
                         nc.tensor.transpose(
-                            flipped[:, i, u, :],
+                            flipped[pair][:, i, u, :],
                             words[:, 256 * g + u : 256 * (g + 1) : 2],
                             ident[:],
                         )
+            for pair in range(PASSES // 2):
                 copy = nc.scalar.copy if pair == 0 else nc.vector.tensor_copy
                 copy(
                     out=grouped_words[:, 2 * pair : 2 * pair + 2, :, :],
-                    in_=flipped[:].rearrange("p i u t -> p i t u"),
+                    in_=flipped[pair][:].rearrange("p i u t -> p i t u"),
                 )
-            nc.vector.quantize_mx(
-                out=x_codes[m][:].bitcast(FP8X4), scales=x_scales[m][:], in_=grouped[:]
-            )
+                begin, end = 2 * pair * P, 2 * (pair + 1) * P
+                nc.vector.quantize_mx(
+                    out=x_codes[m][:, begin:end].bitcast(FP8X4),
+                    scales=x_scales[m][:, begin:end],
+                    in_=grouped[:, 4 * begin : 4 * end],
+                )
 
         def project(m, c):
             acc = psum_acc.tile([P, HEADS_PER_BANK, HEAD], F32, name="acc")
@@ -173,7 +178,7 @@ def tile_qwen3nextattentionforengine_pa_kernel(
                     lhsT=x_codes[m][:, g * P : (g + 1) * P].bitcast(FP8X4),
                     lhsT_scale=x_scales[m][:, g * P : (g + 1) * P],
                     rhs=w_words[c][:, g, :].bitcast(FP4X4),
-                    rhs_scale=w_scales[:, g, c * N_TILE : (c + 1) * N_TILE],
+                    rhs_scale=w_scales[c][:, g, :],
                     start=(g == 0),
                     stop=(g == PASSES - 1),
                 )
@@ -194,9 +199,9 @@ def tile_qwen3nextattentionforengine_pa_kernel(
             )
             return rstd
 
-        def multiply(m, c, acc):
+        def rotate(m, c, acc):
             kind = chunks[c][0]
-            straight = results.tile([P, HEADS_PER_BANK, HEAD], F32, name="straight")
+            straight = products.tile([P, HEADS_PER_BANK, HEAD], F32, name="straight")
             crossed = products.tile([P, HEADS_PER_BANK, HEAD], F32, name="crossed")
             nc.vector.tensor_tensor(
                 out=straight[:],
@@ -213,41 +218,42 @@ def tile_qwen3nextattentionforengine_pa_kernel(
                     .to_broadcast([P, HEADS_PER_BANK, HALF]),
                     op=ALU.mult,
                 )
-            return straight, crossed
-
-        def add(straight, crossed):
-            nc.vector.tensor_tensor(out=straight[:], in0=straight[:], in1=crossed[:], op=ALU.add)
+            rotated = results.tile([P, HEADS_PER_BANK, HEAD], F32, name="rotated")
+            adder = nc.vector if kind == "k" else nc.gpsimd
+            adder.tensor_tensor(out=rotated[:], in0=straight[:], in1=crossed[:], op=ALU.add)
+            return rotated
 
         def scale_and_store(m, c, rotated, rstd):
-            n, rows = chunks[c][2], chunks[c][3]
+            n, tiles = chunks[c][3], chunks[c][4]
             for h in range(HEADS_PER_BANK):
                 nc.scalar.activation(
                     out=rotated[:, h, :], in_=rotated[:, h, :], func=ACT.Copy, scale=rstd[:, h : h + 1]
                 )
             nc.sync.dma_start(
-                out=rows[m * P : (m + 1) * P, n * N_TILE : (n + 1) * N_TILE],
+                out=tiles[m][:, n * N_TILE : (n + 1) * N_TILE],
                 in_=rotated[:].rearrange("p h d -> p (h d)"),
             )
 
         ctx.enter_context(tc.manual_schedule())
 
-        nc.vector.memset(w_scales[:].bitcast(I32), 0)
+        nc.vector.memset(gain_rows[:], 0.0)
+        for c in range(len(chunks)):
+            nc.vector.memset(w_scales[c][:].bitcast(I32), 0)
+        nc.vector.memset(ones[:], 1.0)
         nc.vector.memset(eps[:], EPS)
         make_identity(nc, ident[:])
 
         load_x(0)
-        load_words(0)
-        nc.scalar.dma_start(out=cos_sb[:], in_=cos.rearrange("b (n p) d -> p (b n) d", p=P))
-        nc.scalar.dma_start(out=sin_sb[:], in_=sin.rearrange("b (n p) d -> p (b n) d", p=P))
-        nc.gpsimd.dma_start(out=gain["q"][:], in_=q_norm_w.partition_broadcast(P))
-        nc.gpsimd.dma_start(out=gain["k"][:], in_=k_norm_w.partition_broadcast(P))
-        load_scales(Wq_query_scales, 0, Q_FEATURES)
-        load_words(1)
-        load_words(2)
-        load_words(3)
+        nc.gpsimd.dma_start(out=gain_rows[0:1, 0, :], in_=q_norm_w.unsqueeze(0))
+        nc.gpsimd.dma_start(out=gain_rows[0:1, 1, :], in_=k_norm_w.unsqueeze(0))
+        nc.gpsimd.dma_start(out=cos_sb[:], in_=cos_tiles)
+        nc.gpsimd.dma_start(out=sin_sb[:], in_=sin_tiles)
+        load_chunk(0)
+        load_chunk(1)
+        load_chunk(2)
         load_x(1)
-        load_scales(Wk_scales, Q_FEATURES, K_FEATURES)
-        load_words(4)
+        load_chunk(3)
+        load_chunk(4)
         load_x(2)
         load_x(3)
 
@@ -257,27 +263,31 @@ def tile_qwen3nextattentionforengine_pa_kernel(
         acc = {}
         sum_sq = {}
         rstd = {}
-        straight = {}
-        crossed = {}
+        rotated = {}
 
         prepare_tokens(0)
-        build_tables("q")
-        build_tables("k")
+        spread = psum_acc.tile([P, HEADS_PER_BANK, HEAD], F32, name="spread", tag="acc")
+        nc.tensor.matmul(
+            out=spread[:, 0:2, :].rearrange("p w d -> p (w d)"),
+            lhsT=ones[:],
+            rhs=gain_rows[:].rearrange("p w d -> p (w d)"),
+            start=True,
+            stop=True,
+        )
+        build_tables("q", spread[:, 0, :])
+        build_tables("k", spread[:, 1, :])
         for last in range(-PROJECT_AHEAD, len(banks)):
             first = last + PROJECT_AHEAD
-            second = last + MULTIPLY_AHEAD
-            third = last + ADD_AHEAD
+            middle = last + ROTATE_AHEAD
             if first < len(banks):
                 soon = first + PREPARE_AHEAD
                 if soon % len(chunks) == 0 and soon < len(banks):
                     prepare_tokens(soon // len(chunks))
                 acc[first] = project(banks[first][0], banks[first][1])
                 sum_sq[first] = sum_squares(acc[first])
-            if 0 <= second < len(banks):
-                straight[second], crossed[second] = multiply(banks[second][0], banks[second][1], acc[second])
-            if 0 <= third < len(banks):
-                add(straight[third], crossed[third])
+            if 0 <= middle < len(banks):
+                rotated[middle] = rotate(banks[middle][0], banks[middle][1], acc[middle])
             if last >= 0:
-                scale_and_store(banks[last][0], banks[last][1], straight[last], rstd[last])
+                scale_and_store(banks[last][0], banks[last][1], rotated[last], rstd[last])
             if first < len(banks):
                 rstd[first] = inverse_rms(sum_sq[first])

@@ -28,7 +28,7 @@ K_FEATURES = 512
 FEATURES = Q_FEATURES + K_FEATURES
 EPS = 1e-6
 PROJECT_AHEAD = 4
-ROTATE_AHEAD = 2
+ROTATE_AHEAD = 3
 PREPARE_AHEAD = 2
 
 FLOPS = 2 * TOKENS * HID * FEATURES
@@ -59,8 +59,8 @@ def tile_qwen3nextattentionforengine_pa_kernel(
         keep = ctx.enter_context(tc.tile_pool(name="keep", bufs=1))
         stage = ctx.enter_context(tc.tile_pool(name="stage", bufs=2))
         small = ctx.enter_context(tc.tile_pool(name="small", bufs=8))
-        products = ctx.enter_context(tc.tile_pool(name="products", bufs=3))
-        results = ctx.enter_context(tc.tile_pool(name="results", bufs=6))
+        products = ctx.enter_context(tc.tile_pool(name="products", bufs=5))
+        results = ctx.enter_context(tc.tile_pool(name="results", bufs=10))
         psum_x = ctx.enter_context(tc.psum_pool(name="psum_x", bufs=2))
         psum_acc = ctx.enter_context(tc.psum_pool(name="psum_acc", bufs=6))
 
@@ -80,7 +80,10 @@ def tile_qwen3nextattentionforengine_pa_kernel(
         ]
 
         def load_x(m):
-            nc.sync.dma_start(out=x_sb[m][:], in_=x_tiles[m])
+            for begin in (0, HID // 2):
+                nc.sync.dma_start(
+                    out=x_sb[m][:, begin : begin + HID // 2], in_=x_tiles[m][:, begin : begin + HID // 2]
+                )
 
         def load_chunk(c):
             words, scales, n = chunks[c][1], chunks[c][2], chunks[c][3]

@@ -27,8 +27,8 @@ Q_FEATURES = 2048
 K_FEATURES = 512
 FEATURES = Q_FEATURES + K_FEATURES
 EPS = 1e-6
-PROJECT_AHEAD = 4
-ROTATE_AHEAD = 3
+ROTATE_BEHIND = 2
+ADD_BEHIND = 3
 PREPARE_AHEAD = 2
 
 FLOPS = 2 * TOKENS * HID * FEATURES
@@ -59,8 +59,8 @@ def tile_qwen3nextattentionforengine_pa_kernel(
         keep = ctx.enter_context(tc.tile_pool(name="keep", bufs=1))
         stage = ctx.enter_context(tc.tile_pool(name="stage", bufs=2))
         small = ctx.enter_context(tc.tile_pool(name="small", bufs=8))
-        products = ctx.enter_context(tc.tile_pool(name="products", bufs=5))
-        results = ctx.enter_context(tc.tile_pool(name="results", bufs=10))
+        products = ctx.enter_context(tc.tile_pool(name="products", bufs=4))
+        results = ctx.enter_context(tc.tile_pool(name="results", bufs=6))
         psum_x = ctx.enter_context(tc.psum_pool(name="psum_x", bufs=2))
         psum_acc = ctx.enter_context(tc.psum_pool(name="psum_acc", bufs=6))
 
@@ -108,11 +108,9 @@ def tile_qwen3nextattentionforengine_pa_kernel(
         ident = keep.tile([P, P], F32, name="ident")
         eps = keep.tile([P, 1], F32, name="eps")
         warm = keep.tile([P, 1], F32, name="warm")
-        cos_w = {}
-        sin_w = {}
+        factors = {}
         for kind in ("q", "k"):
-            cos_w[kind] = keep.tile([P, TOKEN_TILES, HEAD], F32, name="cos_w_" + kind)
-            sin_w[kind] = keep.tile([P, TOKEN_TILES, HEAD], F32, name="sin_w_" + kind)
+            factors[kind] = keep.tile([P, TOKEN_TILES, 2, HEAD], F32, name="factors_" + kind)
         x_codes = [
             keep.tile([P, PASSES * P], U32, name="x_codes%d" % m, align_bytes=64)
             for m in range(TOKEN_TILES)
@@ -124,25 +122,24 @@ def tile_qwen3nextattentionforengine_pa_kernel(
         squares = keep.tile([P, HEADS_PER_BANK, HEAD], F32, name="squares")
 
         def build_tables(kind, w):
+            low = w[:, 0:HALF].unsqueeze(1).to_broadcast([P, TOKEN_TILES, HALF])
+            high = w[:, HALF:HEAD].unsqueeze(1).to_broadcast([P, TOKEN_TILES, HALF])
             nc.vector.tensor_tensor(
-                out=cos_w[kind][:],
-                in0=cos_sb[:],
-                in1=w.unsqueeze(1).to_broadcast([P, TOKEN_TILES, HEAD]),
-                op=ALU.mult,
+                out=factors[kind][:, :, 0, 0:HALF], in0=cos_sb[:, :, 0:HALF], in1=low, op=ALU.mult
             )
             nc.vector.scalar_tensor_tensor(
-                out=sin_w[kind][:, :, 0:HALF],
+                out=factors[kind][:, :, 0, HALF:HEAD],
                 in0=sin_sb[:, :, 0:HALF],
                 scalar=-1.0,
-                in1=w[:, HALF:HEAD].unsqueeze(1).to_broadcast([P, TOKEN_TILES, HALF]),
+                in1=high,
                 op0=ALU.mult,
                 op1=ALU.mult,
             )
             nc.vector.tensor_tensor(
-                out=sin_w[kind][:, :, HALF:HEAD],
-                in0=sin_sb[:, :, HALF:HEAD],
-                in1=w[:, 0:HALF].unsqueeze(1).to_broadcast([P, TOKEN_TILES, HALF]),
-                op=ALU.mult,
+                out=factors[kind][:, :, 1, 0:HALF], in0=sin_sb[:, :, HALF:HEAD], in1=low, op=ALU.mult
+            )
+            nc.vector.tensor_tensor(
+                out=factors[kind][:, :, 1, HALF:HEAD], in0=cos_sb[:, :, HALF:HEAD], in1=high, op=ALU.mult
             )
 
         def prepare_tokens(m):
@@ -161,8 +158,7 @@ def tile_qwen3nextattentionforengine_pa_kernel(
                             ident[:],
                         )
             for pair in range(PASSES // 2):
-                copy = nc.scalar.copy if pair == 0 else nc.vector.tensor_copy
-                copy(
+                nc.scalar.copy(
                     out=grouped_words[:, 2 * pair : 2 * pair + 2, :, :],
                     in_=flipped[pair][:].rearrange("p i u t -> p i t u"),
                 )
@@ -202,39 +198,27 @@ def tile_qwen3nextattentionforengine_pa_kernel(
             )
             return rstd
 
-        def rotate(m, c, acc):
+        def rotate(m, c, acc, rstd):
             kind = chunks[c][0]
-            straight = products.tile([P, HEADS_PER_BANK, HEAD], F32, name="straight")
-            crossed = products.tile([P, HEADS_PER_BANK, HEAD], F32, name="crossed")
-            nc.vector.tensor_tensor(
-                out=straight[:],
-                in0=acc[:],
-                in1=cos_w[kind][:, m, :].unsqueeze(1).to_broadcast([P, HEADS_PER_BANK, HEAD]),
-                op=ALU.mult,
-            )
-            for here, there in ((0, HALF), (HALF, 0)):
-                nc.vector.tensor_tensor(
-                    out=crossed[:, :, here : here + HALF],
-                    in0=acc[:, :, there : there + HALF],
-                    in1=sin_w[kind][:, m, here : here + HALF]
-                    .unsqueeze(1)
-                    .to_broadcast([P, HEADS_PER_BANK, HALF]),
-                    op=ALU.mult,
-                )
-            rotated = results.tile([P, HEADS_PER_BANK, HEAD], F32, name="rotated")
-            adder = nc.vector if kind == "k" else nc.gpsimd
-            adder.tensor_tensor(out=rotated[:], in0=straight[:], in1=crossed[:], op=ALU.add)
-            return rotated
-
-        def scale_and_store(m, c, rotated, rstd):
-            n, tiles = chunks[c][3], chunks[c][4]
+            pieces = products.tile([P, 2 * HEADS_PER_BANK, 2, HALF], F32, name="pieces")
             for h in range(HEADS_PER_BANK):
-                nc.scalar.activation(
-                    out=rotated[:, h, :], in_=rotated[:, h, :], func=ACT.Copy, scale=rstd[:, h : h + 1]
+                nc.vector.scalar_tensor_tensor(
+                    out=pieces[:, 2 * h : 2 * h + 2, :, :].rearrange("p x s j -> p x (s j)"),
+                    in0=acc[:, h, :].unsqueeze(1).to_broadcast([P, 2, HEAD]),
+                    scalar=rstd[:, h : h + 1],
+                    in1=factors[kind][:, m, :, :],
+                    op0=ALU.mult,
+                    op1=ALU.mult,
                 )
+            return pieces
+
+        def add_and_store(m, c, pieces):
+            n, tiles = chunks[c][3], chunks[c][4]
+            rotated = results.tile([P, 2 * HEADS_PER_BANK, HALF], F32, name="rotated")
+            nc.gpsimd.tensor_tensor(out=rotated[:], in0=pieces[:, :, 0, :], in1=pieces[:, :, 1, :], op=ALU.add)
             nc.sync.dma_start(
                 out=tiles[m][:, n * N_TILE : (n + 1) * N_TILE],
-                in_=rotated[:].rearrange("p h d -> p (h d)"),
+                in_=rotated[:].rearrange("p x j -> p (x j)"),
             )
 
         ctx.enter_context(tc.manual_schedule())
@@ -266,7 +250,7 @@ def tile_qwen3nextattentionforengine_pa_kernel(
         acc = {}
         sum_sq = {}
         rstd = {}
-        rotated = {}
+        pieces = {}
 
         prepare_tokens(0)
         spread = psum_acc.tile([P, HEADS_PER_BANK, HEAD], F32, name="spread", tag="acc")
@@ -279,18 +263,17 @@ def tile_qwen3nextattentionforengine_pa_kernel(
         )
         build_tables("q", spread[:, 0, :])
         build_tables("k", spread[:, 1, :])
-        for last in range(-PROJECT_AHEAD, len(banks)):
-            first = last + PROJECT_AHEAD
-            middle = last + ROTATE_AHEAD
+        for first in range(len(banks) + ADD_BEHIND):
+            middle = first - ROTATE_BEHIND
+            last = first - ADD_BEHIND
             if first < len(banks):
                 soon = first + PREPARE_AHEAD
                 if soon % len(chunks) == 0 and soon < len(banks):
                     prepare_tokens(soon // len(chunks))
                 acc[first] = project(banks[first][0], banks[first][1])
                 sum_sq[first] = sum_squares(acc[first])
-            if 0 <= middle < len(banks):
-                rotated[middle] = rotate(banks[middle][0], banks[middle][1], acc[middle])
-            if last >= 0:
-                scale_and_store(banks[last][0], banks[last][1], rotated[last], rstd[last])
-            if first < len(banks):
                 rstd[first] = inverse_rms(sum_sq[first])
+            if 0 <= middle < len(banks):
+                pieces[middle] = rotate(banks[middle][0], banks[middle][1], acc[middle], rstd[middle])
+            if 0 <= last:
+                add_and_store(banks[last][0], banks[last][1], pieces[last])

@@ -30,6 +30,8 @@ EPS = 1e-6
 ROTATE_BEHIND = 2
 ADD_BEHIND = 3
 PREPARE_AHEAD = 2
+LEAD = 3
+VECTOR_ADDS = 2
 
 FLOPS = 2 * TOKENS * HID * FEATURES
 
@@ -87,6 +89,12 @@ def tile_qwen3nextattentionforengine_pa_kernel(
 
         def load_chunk(c):
             words, scales, n = chunks[c][1], chunks[c][2], chunks[c][3]
+            by_partition = words.bitcast(I32).rearrange("g p w -> p g w")
+            width = 2 * N_TILE // 4
+            nc.sync.dma_start(
+                out=w_words[c][:].bitcast(I32),
+                in_=by_partition[:, :, n * width : (n + 1) * width],
+            )
             by_row = scales.bitcast(I32).rearrange("g (Q r) w -> r Q g w", r=4)
             width = N_TILE // 4
             for r in range(4):
@@ -94,12 +102,6 @@ def tile_qwen3nextattentionforengine_pa_kernel(
                     out=w_scales[c][r:P:32, :, :].bitcast(I32),
                     in_=by_row[r][:, :, n * width : (n + 1) * width],
                 )
-            by_partition = words.bitcast(I32).rearrange("g p w -> p g w")
-            width = 2 * N_TILE // 4
-            nc.sync.dma_start(
-                out=w_words[c][:].bitcast(I32),
-                in_=by_partition[:, :, n * width : (n + 1) * width],
-            )
 
         cos_sb = keep.tile([P, TOKEN_TILES, HEAD], BF16, name="cos_sb")
         sin_sb = keep.tile([P, TOKEN_TILES, HEAD], BF16, name="sin_sb")
@@ -142,7 +144,7 @@ def tile_qwen3nextattentionforengine_pa_kernel(
                 out=factors[kind][:, :, 1, HALF:HEAD], in0=cos_sb[:, :, HALF:HEAD], in1=high, op=ALU.mult
             )
 
-        def prepare_tokens(m):
+        def flip_tokens(m):
             words = x_sb[m][:].bitcast(F32)
             grouped = stage.tile([P, PASSES * P * 4], BF16, name="grouped", align_bytes=64)
             grouped_words = grouped[:].bitcast(F32).rearrange("p (g t u) -> p g t u", g=PASSES, u=2)
@@ -162,6 +164,10 @@ def tile_qwen3nextattentionforengine_pa_kernel(
                     out=grouped_words[:, 2 * pair : 2 * pair + 2, :, :],
                     in_=flipped[pair][:].rearrange("p i u t -> p i t u"),
                 )
+            return grouped
+
+        def quantise_tokens(m, grouped):
+            for pair in range(PASSES // 2):
                 begin, end = 2 * pair * P, 2 * (pair + 1) * P
                 nc.vector.quantize_mx(
                     out=x_codes[m][:, begin:end].bitcast(FP8X4),
@@ -212,10 +218,10 @@ def tile_qwen3nextattentionforengine_pa_kernel(
                 )
             return pieces
 
-        def add_and_store(m, c, pieces):
+        def add_and_store(adder, m, c, pieces):
             n, tiles = chunks[c][3], chunks[c][4]
             rotated = results.tile([P, 2 * HEADS_PER_BANK, HALF], F32, name="rotated")
-            nc.gpsimd.tensor_tensor(out=rotated[:], in0=pieces[:, :, 0, :], in1=pieces[:, :, 1, :], op=ALU.add)
+            adder.tensor_tensor(out=rotated[:], in0=pieces[:, :, 0, :], in1=pieces[:, :, 1, :], op=ALU.add)
             nc.sync.dma_start(
                 out=tiles[m][:, n * N_TILE : (n + 1) * N_TILE],
                 in_=rotated[:].rearrange("p x j -> p (x j)"),
@@ -231,14 +237,14 @@ def tile_qwen3nextattentionforengine_pa_kernel(
         make_identity(nc, ident[:])
 
         load_x(0)
-        nc.gpsimd.dma_start(out=gain_rows[0:1, 0, :], in_=q_norm_w.unsqueeze(0))
-        nc.gpsimd.dma_start(out=gain_rows[0:1, 1, :], in_=k_norm_w.unsqueeze(0))
+        nc.scalar.dma_start(out=gain_rows[0:1, 0, :], in_=q_norm_w.unsqueeze(0))
+        nc.scalar.dma_start(out=gain_rows[0:1, 1, :], in_=k_norm_w.unsqueeze(0))
         nc.gpsimd.dma_start(out=cos_sb[:], in_=cos_tiles)
         nc.gpsimd.dma_start(out=sin_sb[:], in_=sin_tiles)
         load_chunk(0)
         load_chunk(1)
-        load_chunk(2)
         load_x(1)
+        load_chunk(2)
         load_chunk(3)
         load_chunk(4)
         load_x(2)
@@ -246,13 +252,17 @@ def tile_qwen3nextattentionforengine_pa_kernel(
 
         nc.scalar.activation(out=warm[:], in_=eps[:], func=ACT.Abs_reciprocal_sqrt)
 
-        banks = [(m, c) for m in range(TOKEN_TILES) for c in range(len(chunks))]
+        banks = [(0, c) for c in range(LEAD)] + [(1, c) for c in range(LEAD)]
+        banks.extend([(m, c) for c in range(LEAD, len(chunks)) for m in (0, 1)])
+        banks.extend([(m, c) for m in (2, 3) for c in range(len(chunks))])
+        first_bank = dict([(m, min([i for i in range(len(banks)) if banks[i][0] == m])) for m in range(TOKEN_TILES)])
+        grouped = {}
         acc = {}
         sum_sq = {}
         rstd = {}
         pieces = {}
 
-        prepare_tokens(0)
+        quantise_tokens(0, flip_tokens(0))
         spread = psum_acc.tile([P, HEADS_PER_BANK, HEAD], F32, name="spread", tag="acc")
         nc.tensor.matmul(
             out=spread[:, 0:2, :].rearrange("p w d -> p (w d)"),
@@ -267,13 +277,16 @@ def tile_qwen3nextattentionforengine_pa_kernel(
             middle = first - ROTATE_BEHIND
             last = first - ADD_BEHIND
             if first < len(banks):
-                soon = first + PREPARE_AHEAD
-                if soon % len(chunks) == 0 and soon < len(banks):
-                    prepare_tokens(soon // len(chunks))
+                for m in range(1, TOKEN_TILES):
+                    if first_bank[m] == first + PREPARE_AHEAD:
+                        grouped[m] = flip_tokens(m)
+                    if first_bank[m] == first:
+                        quantise_tokens(m, grouped[m])
                 acc[first] = project(banks[first][0], banks[first][1])
                 sum_sq[first] = sum_squares(acc[first])
                 rstd[first] = inverse_rms(sum_sq[first])
             if 0 <= middle < len(banks):
                 pieces[middle] = rotate(banks[middle][0], banks[middle][1], acc[middle], rstd[middle])
             if 0 <= last:
-                add_and_store(banks[last][0], banks[last][1], pieces[last])
+                adder = nc.vector if last >= len(banks) - VECTOR_ADDS else nc.gpsimd
+                add_and_store(adder, banks[last][0], banks[last][1], pieces[last])

@@ -31,6 +31,8 @@ ROTATE_BEHIND = 2
 ADD_BEHIND = 3
 PREPARE_AHEAD = 2
 LEAD = 3
+WARM_BEFORE = 4
+WARM_BETWEEN = 2
 VECTOR_ADDS = 2
 
 FLOPS = 2 * TOKENS * HID * FEATURES
@@ -106,7 +108,9 @@ def tile_qwen3nextattentionforengine_pa_kernel(
         cos_sb = keep.tile([P, TOKEN_TILES, HEAD], BF16, name="cos_sb")
         sin_sb = keep.tile([P, TOKEN_TILES, HEAD], BF16, name="sin_sb")
         ones = keep.tile([P, P], BF16, name="ones")
+        idle_rhs = keep.tile([P, N_TILE], BF16, name="idle_rhs")
         gain_rows = keep.tile([P, 2, HEAD], BF16, name="gain_rows")
+        w_key = keep.tile([P, HEAD + HALF], F32, name="w_key")
         ident = keep.tile([P, P], F32, name="ident")
         eps = keep.tile([P, 1], F32, name="eps")
         warm = keep.tile([P, 1], F32, name="warm")
@@ -123,26 +127,31 @@ def tile_qwen3nextattentionforengine_pa_kernel(
         ]
         squares = keep.tile([P, HEADS_PER_BANK, HEAD], F32, name="squares")
 
-        def build_tables(kind, w):
-            low = w[:, 0:HALF].unsqueeze(1).to_broadcast([P, TOKEN_TILES, HALF])
-            high = w[:, HALF:HEAD].unsqueeze(1).to_broadcast([P, TOKEN_TILES, HALF])
-            nc.vector.tensor_tensor(
-                out=factors[kind][:, :, 0, 0:HALF], in0=cos_sb[:, :, 0:HALF], in1=low, op=ALU.mult
-            )
-            nc.vector.scalar_tensor_tensor(
-                out=factors[kind][:, :, 0, HALF:HEAD],
-                in0=sin_sb[:, :, 0:HALF],
-                scalar=-1.0,
-                in1=high,
-                op0=ALU.mult,
-                op1=ALU.mult,
-            )
-            nc.vector.tensor_tensor(
-                out=factors[kind][:, :, 1, 0:HALF], in0=sin_sb[:, :, HALF:HEAD], in1=low, op=ALU.mult
-            )
-            nc.vector.tensor_tensor(
+        def build_tables(engine, kind, w, minus_w_high):
+            shape = [P, TOKEN_TILES, HALF]
+            low = w[:, 0:HALF].unsqueeze(1).to_broadcast(shape)
+            high = w[:, HALF:HEAD].unsqueeze(1).to_broadcast(shape)
+            engine.tensor_tensor(out=factors[kind][:, :, 0, 0:HALF], in0=cos_sb[:, :, 0:HALF], in1=low, op=ALU.mult)
+            engine.tensor_tensor(
                 out=factors[kind][:, :, 1, HALF:HEAD], in0=cos_sb[:, :, HALF:HEAD], in1=high, op=ALU.mult
             )
+            engine.tensor_tensor(out=factors[kind][:, :, 1, 0:HALF], in0=sin_sb[:, :, HALF:HEAD], in1=low, op=ALU.mult)
+            if minus_w_high is None:
+                engine.scalar_tensor_tensor(
+                    out=factors[kind][:, :, 0, HALF:HEAD],
+                    in0=sin_sb[:, :, 0:HALF],
+                    scalar=-1.0,
+                    in1=high,
+                    op0=ALU.mult,
+                    op1=ALU.mult,
+                )
+            else:
+                engine.tensor_tensor(
+                    out=factors[kind][:, :, 0, HALF:HEAD],
+                    in0=sin_sb[:, :, 0:HALF],
+                    in1=minus_w_high.unsqueeze(1).to_broadcast(shape),
+                    op=ALU.mult,
+                )
 
         def flip_tokens(m):
             words = x_sb[m][:].bitcast(F32)
@@ -166,9 +175,10 @@ def tile_qwen3nextattentionforengine_pa_kernel(
                 )
             return grouped
 
-        def quantise_tokens(m, grouped):
-            for pair in range(PASSES // 2):
-                begin, end = 2 * pair * P, 2 * (pair + 1) * P
+        def quantise_tokens(m, grouped, calls):
+            width = PASSES * P // calls
+            for begin in range(0, PASSES * P, width):
+                end = begin + width
                 nc.vector.quantize_mx(
                     out=x_codes[m][:, begin:end].bitcast(FP8X4),
                     scales=x_scales[m][:, begin:end],
@@ -229,12 +239,20 @@ def tile_qwen3nextattentionforengine_pa_kernel(
 
         ctx.enter_context(tc.manual_schedule())
 
+        nc.vector.memset(ones[:], 1.0)
+        nc.vector.memset(idle_rhs[:], 0.0)
         nc.vector.memset(gain_rows[:], 0.0)
         for c in range(len(chunks)):
             nc.vector.memset(w_scales[c][:].bitcast(I32), 0)
-        nc.vector.memset(ones[:], 1.0)
         nc.vector.memset(eps[:], EPS)
         make_identity(nc, ident[:])
+
+        def idle_matmuls(count):
+            idle = psum_acc.tile([P, HEADS_PER_BANK, HEAD], F32, name="idle", tag="acc")
+            for i in range(count):
+                nc.tensor.matmul(
+                    out=idle[:].rearrange("p h d -> p (h d)"), lhsT=ones[:], rhs=idle_rhs[:], start=True, stop=True
+                )
 
         load_x(0)
         nc.scalar.dma_start(out=gain_rows[0:1, 0, :], in_=q_norm_w.unsqueeze(0))
@@ -262,7 +280,8 @@ def tile_qwen3nextattentionforengine_pa_kernel(
         rstd = {}
         pieces = {}
 
-        quantise_tokens(0, flip_tokens(0))
+        idle_matmuls(WARM_BEFORE)
+        quantise_tokens(0, flip_tokens(0), 2)
         spread = psum_acc.tile([P, HEADS_PER_BANK, HEAD], F32, name="spread", tag="acc")
         nc.tensor.matmul(
             out=spread[:, 0:2, :].rearrange("p w d -> p (w d)"),
@@ -271,8 +290,11 @@ def tile_qwen3nextattentionforengine_pa_kernel(
             start=True,
             stop=True,
         )
-        build_tables("q", spread[:, 0, :])
-        build_tables("k", spread[:, 1, :])
+        idle_matmuls(WARM_BETWEEN)
+        build_tables(nc.vector, "q", spread[:, 0, :], None)
+        nc.scalar.copy(out=w_key[:, 0:HEAD], in_=spread[:, 1, :])
+        nc.scalar.activation(out=w_key[:, HEAD : HEAD + HALF], in_=spread[:, 1, HALF:HEAD], func=ACT.Copy, scale=-1.0)
+        build_tables(nc.gpsimd, "k", w_key[:, 0:HEAD], w_key[:, HEAD : HEAD + HALF])
         for first in range(len(banks) + ADD_BEHIND):
             middle = first - ROTATE_BEHIND
             last = first - ADD_BEHIND
@@ -281,7 +303,7 @@ def tile_qwen3nextattentionforengine_pa_kernel(
                     if first_bank[m] == first + PREPARE_AHEAD:
                         grouped[m] = flip_tokens(m)
                     if first_bank[m] == first:
-                        quantise_tokens(m, grouped[m])
+                        quantise_tokens(m, grouped[m], 1)
                 acc[first] = project(banks[first][0], banks[first][1])
                 sum_sq[first] = sum_squares(acc[first])
                 rstd[first] = inverse_rms(sum_sq[first])

@@ -291,18 +291,19 @@ def tile_qwen3nextattentionforengine_pa_kernel(
             stop=True,
         )
         idle_matmuls(WARM_BETWEEN)
-        build_tables(nc.vector, "q", spread[:, 0, :], None)
         nc.scalar.copy(out=w_key[:, 0:HEAD], in_=spread[:, 1, :])
         nc.scalar.activation(out=w_key[:, HEAD : HEAD + HALF], in_=spread[:, 1, HALF:HEAD], func=ACT.Copy, scale=-1.0)
+        build_tables(nc.vector, "q", spread[:, 0, :], None)
         build_tables(nc.gpsimd, "k", w_key[:, 0:HEAD], w_key[:, HEAD : HEAD + HALF])
         for first in range(len(banks) + ADD_BEHIND):
             middle = first - ROTATE_BEHIND
             last = first - ADD_BEHIND
             if first < len(banks):
                 for m in range(1, TOKEN_TILES):
-                    if first_bank[m] == first + PREPARE_AHEAD:
+                    early = 0 if m == 1 else 1
+                    if first_bank[m] == first + PREPARE_AHEAD + early:
                         grouped[m] = flip_tokens(m)
-                    if first_bank[m] == first:
+                    if first_bank[m] == first + early:
                         quantise_tokens(m, grouped[m], 1)
                 acc[first] = project(banks[first][0], banks[first][1])
                 sum_sq[first] = sum_squares(acc[first])

@@ -29,8 +29,8 @@ FEATURES = Q_FEATURES + K_FEATURES
 EPS = 1e-6
 ROTATE_BEHIND = 2
 ADD_BEHIND = 3
-PREPARE_AHEAD = 2
-LEAD = 3
+PREPARE_AHEAD = 3
+QUANTISE_AHEAD = 1
 WARM_BEFORE = 4
 WARM_BETWEEN = 2
 VECTOR_ADDS = 2
@@ -83,11 +83,10 @@ def tile_qwen3nextattentionforengine_pa_kernel(
             for c in range(len(chunks))
         ]
 
-        def load_x(m):
-            for begin in (0, HID // 2):
-                nc.sync.dma_start(
-                    out=x_sb[m][:, begin : begin + HID // 2], in_=x_tiles[m][:, begin : begin + HID // 2]
-                )
+        def load_x(m, parts):
+            width = HID // parts
+            for begin in range(0, HID, width):
+                nc.sync.dma_start(out=x_sb[m][:, begin : begin + width], in_=x_tiles[m][:, begin : begin + width])
 
         def load_chunk(c):
             words, scales, n = chunks[c][1], chunks[c][2], chunks[c][3]
@@ -254,24 +253,20 @@ def tile_qwen3nextattentionforengine_pa_kernel(
                     out=idle[:].rearrange("p h d -> p (h d)"), lhsT=ones[:], rhs=idle_rhs[:], start=True, stop=True
                 )
 
-        load_x(0)
+        load_x(0, 2)
+        load_x(1, 1)
         nc.scalar.dma_start(out=gain_rows[0:1, 0, :], in_=q_norm_w.unsqueeze(0))
         nc.scalar.dma_start(out=gain_rows[0:1, 1, :], in_=k_norm_w.unsqueeze(0))
         nc.gpsimd.dma_start(out=cos_sb[:], in_=cos_tiles)
         nc.gpsimd.dma_start(out=sin_sb[:], in_=sin_tiles)
-        load_chunk(0)
-        load_chunk(1)
-        load_x(1)
-        load_chunk(2)
-        load_chunk(3)
-        load_chunk(4)
-        load_x(2)
-        load_x(3)
+        for c in range(len(chunks)):
+            load_chunk(c)
+        load_x(2, 2)
+        load_x(3, 2)
 
         nc.scalar.activation(out=warm[:], in_=eps[:], func=ACT.Abs_reciprocal_sqrt)
 
-        banks = [(0, c) for c in range(LEAD)] + [(1, c) for c in range(LEAD)]
-        banks.extend([(m, c) for c in range(LEAD, len(chunks)) for m in (0, 1)])
+        banks = [(m, c) for c in range(len(chunks)) for m in (0, 1)]
         banks.extend([(m, c) for m in (2, 3) for c in range(len(chunks))])
         first_bank = dict([(m, min([i for i in range(len(banks)) if banks[i][0] == m])) for m in range(TOKEN_TILES)])
         grouped = {}
@@ -295,15 +290,15 @@ def tile_qwen3nextattentionforengine_pa_kernel(
         nc.scalar.activation(out=w_key[:, HEAD : HEAD + HALF], in_=spread[:, 1, HALF:HEAD], func=ACT.Copy, scale=-1.0)
         build_tables(nc.vector, "q", spread[:, 0, :], None)
         build_tables(nc.gpsimd, "k", w_key[:, 0:HEAD], w_key[:, HEAD : HEAD + HALF])
+        quantise_tokens(1, flip_tokens(1), 1)
         for first in range(len(banks) + ADD_BEHIND):
             middle = first - ROTATE_BEHIND
             last = first - ADD_BEHIND
             if first < len(banks):
-                for m in range(1, TOKEN_TILES):
-                    early = 0 if m == 1 else 1
-                    if first_bank[m] == first + PREPARE_AHEAD + early:
+                for m in (2, 3):
+                    if first_bank[m] == first + PREPARE_AHEAD:
                         grouped[m] = flip_tokens(m)
-                    if first_bank[m] == first + early:
+                    if first_bank[m] == first + QUANTISE_AHEAD:
                         quantise_tokens(m, grouped[m], 1)
                 acc[first] = project(banks[first][0], banks[first][1])
                 sum_sq[first] = sum_squares(acc[first])

@@ -31,7 +31,7 @@ ROTATE_BEHIND = 2
 ADD_BEHIND = 3
 PREPARE_AHEAD = 3
 QUANTISE_AHEAD = 1
-WARM_BEFORE = 4
+WARM_BEFORE = 3
 WARM_BETWEEN = 2
 VECTOR_ADDS = 2
 
@@ -88,14 +88,17 @@ def tile_qwen3nextattentionforengine_pa_kernel(
             for begin in range(0, HID, width):
                 nc.sync.dma_start(out=x_sb[m][:, begin : begin + width], in_=x_tiles[m][:, begin : begin + width])
 
-        def load_chunk(c):
-            words, scales, n = chunks[c][1], chunks[c][2], chunks[c][3]
+        def load_words(c):
+            words, n = chunks[c][1], chunks[c][3]
             by_partition = words.bitcast(I32).rearrange("g p w -> p g w")
             width = 2 * N_TILE // 4
             nc.sync.dma_start(
                 out=w_words[c][:].bitcast(I32),
                 in_=by_partition[:, :, n * width : (n + 1) * width],
             )
+
+        def load_scales(c):
+            scales, n = chunks[c][2], chunks[c][3]
             by_row = scales.bitcast(I32).rearrange("g (Q r) w -> r Q g w", r=4)
             width = N_TILE // 4
             for r in range(4):
@@ -107,7 +110,6 @@ def tile_qwen3nextattentionforengine_pa_kernel(
         cos_sb = keep.tile([P, TOKEN_TILES, HEAD], BF16, name="cos_sb")
         sin_sb = keep.tile([P, TOKEN_TILES, HEAD], BF16, name="sin_sb")
         ones = keep.tile([P, P], BF16, name="ones")
-        idle_rhs = keep.tile([P, N_TILE], BF16, name="idle_rhs")
         gain_rows = keep.tile([P, 2, HEAD], BF16, name="gain_rows")
         w_key = keep.tile([P, HEAD + HALF], F32, name="w_key")
         ident = keep.tile([P, P], F32, name="ident")
@@ -126,7 +128,7 @@ def tile_qwen3nextattentionforengine_pa_kernel(
         ]
         squares = keep.tile([P, HEADS_PER_BANK, HEAD], F32, name="squares")
 
-        def build_tables(engine, kind, w, minus_w_high):
+        def build_cos_tables(engine, kind, w):
             shape = [P, TOKEN_TILES, HALF]
             low = w[:, 0:HALF].unsqueeze(1).to_broadcast(shape)
             high = w[:, HALF:HEAD].unsqueeze(1).to_broadcast(shape)
@@ -134,6 +136,11 @@ def tile_qwen3nextattentionforengine_pa_kernel(
             engine.tensor_tensor(
                 out=factors[kind][:, :, 1, HALF:HEAD], in0=cos_sb[:, :, HALF:HEAD], in1=high, op=ALU.mult
             )
+
+        def build_sin_tables(engine, kind, w, minus_w_high):
+            shape = [P, TOKEN_TILES, HALF]
+            low = w[:, 0:HALF].unsqueeze(1).to_broadcast(shape)
+            high = w[:, HALF:HEAD].unsqueeze(1).to_broadcast(shape)
             engine.tensor_tensor(out=factors[kind][:, :, 1, 0:HALF], in0=sin_sb[:, :, HALF:HEAD], in1=low, op=ALU.mult)
             if minus_w_high is None:
                 engine.scalar_tensor_tensor(
@@ -238,29 +245,36 @@ def tile_qwen3nextattentionforengine_pa_kernel(
 
         ctx.enter_context(tc.manual_schedule())
 
-        nc.vector.memset(ones[:], 1.0)
-        nc.vector.memset(idle_rhs[:], 0.0)
         nc.vector.memset(gain_rows[:], 0.0)
-        for c in range(len(chunks)):
-            nc.vector.memset(w_scales[c][:].bitcast(I32), 0)
+        nc.vector.memset(ones[:], 1.0)
+        nc.vector.memset(w_scales[0][:].bitcast(I32), 0)
         nc.vector.memset(eps[:], EPS)
+        for c in range(1, len(chunks)):
+            nc.vector.memset(w_scales[c][:].bitcast(I32), 0)
         make_identity(nc, ident[:])
 
         def idle_matmuls(count):
             idle = psum_acc.tile([P, HEADS_PER_BANK, HEAD], F32, name="idle", tag="acc")
             for i in range(count):
                 nc.tensor.matmul(
-                    out=idle[:].rearrange("p h d -> p (h d)"), lhsT=ones[:], rhs=idle_rhs[:], start=True, stop=True
+                    out=idle[:],
+                    lhsT=ones[:],
+                    rhs=ones[:].unsqueeze(1).to_broadcast([P, HEADS_PER_BANK, HEAD]),
+                    start=True,
+                    stop=True,
                 )
 
         load_x(0, 2)
+        nc.sync.dma_start(out=gain_rows[0:1, 0, :], in_=q_norm_w.unsqueeze(0))
+        nc.sync.dma_start(out=gain_rows[0:1, 1, :], in_=k_norm_w.unsqueeze(0))
         load_x(1, 1)
-        nc.scalar.dma_start(out=gain_rows[0:1, 0, :], in_=q_norm_w.unsqueeze(0))
-        nc.scalar.dma_start(out=gain_rows[0:1, 1, :], in_=k_norm_w.unsqueeze(0))
+        load_words(0)
+        load_scales(0)
         nc.gpsimd.dma_start(out=cos_sb[:], in_=cos_tiles)
         nc.gpsimd.dma_start(out=sin_sb[:], in_=sin_tiles)
-        for c in range(len(chunks)):
-            load_chunk(c)
+        for c in range(1, len(chunks)):
+            load_words(c)
+            load_scales(c)
         load_x(2, 2)
         load_x(3, 2)
 
@@ -288,9 +302,11 @@ def tile_qwen3nextattentionforengine_pa_kernel(
         idle_matmuls(WARM_BETWEEN)
         nc.scalar.copy(out=w_key[:, 0:HEAD], in_=spread[:, 1, :])
         nc.scalar.activation(out=w_key[:, HEAD : HEAD + HALF], in_=spread[:, 1, HALF:HEAD], func=ACT.Copy, scale=-1.0)
-        build_tables(nc.vector, "q", spread[:, 0, :], None)
-        build_tables(nc.gpsimd, "k", w_key[:, 0:HEAD], w_key[:, HEAD : HEAD + HALF])
+        build_cos_tables(nc.vector, "q", spread[:, 0, :])
         quantise_tokens(1, flip_tokens(1), 1)
+        build_sin_tables(nc.vector, "q", spread[:, 0, :], None)
+        build_cos_tables(nc.gpsimd, "k", w_key[:, 0:HEAD])
+        build_sin_tables(nc.gpsimd, "k", w_key[:, 0:HEAD], w_key[:, HEAD : HEAD + HALF])
         for first in range(len(banks) + ADD_BEHIND):
             middle = first - ROTATE_BEHIND
             last = first - ADD_BEHIND

@@ -32,7 +32,8 @@ ADD_BEHIND = 3
 PREPARE_AHEAD = 3
 QUANTISE_AHEAD = 1
 WARM_BEFORE = 3
-WARM_BETWEEN = 2
+WARM_BETWEEN = 1
+EAGER_BANKS = 4
 VECTOR_ADDS = 2
 
 FLOPS = 2 * TOKENS * HID * FEATURES
@@ -110,7 +111,9 @@ def tile_qwen3nextattentionforengine_pa_kernel(
         cos_sb = keep.tile([P, TOKEN_TILES, HEAD], BF16, name="cos_sb")
         sin_sb = keep.tile([P, TOKEN_TILES, HEAD], BF16, name="sin_sb")
         ones = keep.tile([P, P], BF16, name="ones")
-        gain_rows = keep.tile([P, 2, HEAD], BF16, name="gain_rows")
+        gain_rows = {}
+        for kind in ("q", "k"):
+            gain_rows[kind] = keep.tile([P, HEAD], BF16, name="gain_rows_" + kind)
         w_key = keep.tile([P, HEAD + HALF], F32, name="w_key")
         ident = keep.tile([P, P], F32, name="ident")
         eps = keep.tile([P, 1], F32, name="eps")
@@ -159,13 +162,13 @@ def tile_qwen3nextattentionforengine_pa_kernel(
                     op=ALU.mult,
                 )
 
-        def flip_tokens(m):
+        def flip_tokens(m, pool, tag):
             words = x_sb[m][:].bitcast(F32)
             grouped = stage.tile([P, PASSES * P * 4], BF16, name="grouped", align_bytes=64)
             grouped_words = grouped[:].bitcast(F32).rearrange("p (g t u) -> p g t u", g=PASSES, u=2)
             flipped = []
             for pair in range(PASSES // 2):
-                flipped.append(psum_x.tile([P, 2, 2, P], F32, name="flipped"))
+                flipped.append(pool.tile([P, 2, 2, P], F32, name="flipped", tag=tag))
                 for i in range(2):
                     g = 2 * pair + i
                     for u in range(2):
@@ -205,19 +208,22 @@ def tile_qwen3nextattentionforengine_pa_kernel(
                 )
             return acc
 
-        def sum_squares(acc):
+        def inverse_rms(acc, group):
             sum_sq = small.tile([P, HEADS_PER_BANK], F32, name="sum_sq")
-            for h in range(HEADS_PER_BANK):
-                nc.scalar.activation(
-                    out=squares[:, h, :], in_=acc[:, h, :], func=ACT.Square, accum_out=sum_sq[:, h : h + 1]
-                )
-            return sum_sq
-
-        def inverse_rms(sum_sq):
             rstd = small.tile([P, HEADS_PER_BANK], F32, name="rstd")
-            nc.scalar.activation(
-                out=rstd[:], in_=sum_sq[:], func=ACT.Abs_reciprocal_sqrt, scale=1.0 / HEAD, bias=eps[:, 0:1]
-            )
+            for begin in range(0, HEADS_PER_BANK, group):
+                end = begin + group
+                for h in range(begin, end):
+                    nc.scalar.activation(
+                        out=squares[:, h, :], in_=acc[:, h, :], func=ACT.Square, accum_out=sum_sq[:, h : h + 1]
+                    )
+                nc.scalar.activation(
+                    out=rstd[:, begin:end],
+                    in_=sum_sq[:, begin:end],
+                    func=ACT.Abs_reciprocal_sqrt,
+                    scale=1.0 / HEAD,
+                    bias=eps[:, 0:1],
+                )
             return rstd
 
         def rotate(m, c, acc, rstd):
@@ -245,8 +251,9 @@ def tile_qwen3nextattentionforengine_pa_kernel(
 
         ctx.enter_context(tc.manual_schedule())
 
-        nc.vector.memset(gain_rows[:], 0.0)
+        nc.vector.memset(gain_rows["q"][:], 0.0)
         nc.vector.memset(ones[:], 1.0)
+        nc.vector.memset(gain_rows["k"][:], 0.0)
         nc.vector.memset(w_scales[0][:].bitcast(I32), 0)
         nc.vector.memset(eps[:], EPS)
         for c in range(1, len(chunks)):
@@ -264,14 +271,14 @@ def tile_qwen3nextattentionforengine_pa_kernel(
                     stop=True,
                 )
 
-        load_x(0, 2)
-        nc.sync.dma_start(out=gain_rows[0:1, 0, :], in_=q_norm_w.unsqueeze(0))
-        nc.sync.dma_start(out=gain_rows[0:1, 1, :], in_=k_norm_w.unsqueeze(0))
+        load_x(0, 1)
+        nc.sync.dma_start(out=gain_rows["q"][0:1, :], in_=q_norm_w.unsqueeze(0))
+        nc.gpsimd.dma_start(out=gain_rows["k"][0:1, :], in_=k_norm_w.unsqueeze(0))
         load_x(1, 1)
         load_words(0)
         load_scales(0)
-        nc.gpsimd.dma_start(out=cos_sb[:], in_=cos_tiles)
-        nc.gpsimd.dma_start(out=sin_sb[:], in_=sin_tiles)
+        nc.sync.dma_start(out=cos_sb[:], in_=cos_tiles)
+        nc.sync.dma_start(out=sin_sb[:], in_=sin_tiles)
         for c in range(1, len(chunks)):
             load_words(c)
             load_scales(c)
@@ -285,26 +292,22 @@ def tile_qwen3nextattentionforengine_pa_kernel(
         first_bank = dict([(m, min([i for i in range(len(banks)) if banks[i][0] == m])) for m in range(TOKEN_TILES)])
         grouped = {}
         acc = {}
-        sum_sq = {}
         rstd = {}
         pieces = {}
 
         idle_matmuls(WARM_BEFORE)
-        quantise_tokens(0, flip_tokens(0), 2)
-        spread = psum_acc.tile([P, HEADS_PER_BANK, HEAD], F32, name="spread", tag="acc")
-        nc.tensor.matmul(
-            out=spread[:, 0:2, :].rearrange("p w d -> p (w d)"),
-            lhsT=ones[:],
-            rhs=gain_rows[:].rearrange("p w d -> p (w d)"),
-            start=True,
-            stop=True,
-        )
+        quantise_tokens(0, flip_tokens(0, psum_x, "x"), 2)
+        x1_grouped = flip_tokens(1, psum_acc, "acc")
+        spread = {}
+        for kind in ("q", "k"):
+            spread[kind] = psum_acc.tile([P, HEADS_PER_BANK, HEAD], F32, name="spread", tag="acc")
+            nc.tensor.matmul(out=spread[kind][:, 0, :], lhsT=ones[:], rhs=gain_rows[kind][:], start=True, stop=True)
         idle_matmuls(WARM_BETWEEN)
-        nc.scalar.copy(out=w_key[:, 0:HEAD], in_=spread[:, 1, :])
-        nc.scalar.activation(out=w_key[:, HEAD : HEAD + HALF], in_=spread[:, 1, HALF:HEAD], func=ACT.Copy, scale=-1.0)
-        build_cos_tables(nc.vector, "q", spread[:, 0, :])
-        quantise_tokens(1, flip_tokens(1), 1)
-        build_sin_tables(nc.vector, "q", spread[:, 0, :], None)
+        nc.scalar.copy(out=w_key[:, 0:HEAD], in_=spread["k"][:, 0, :])
+        nc.scalar.activation(out=w_key[:, HEAD : HEAD + HALF], in_=spread["k"][:, 0, HALF:HEAD], func=ACT.Copy, scale=-1.0)
+        build_cos_tables(nc.vector, "q", spread["q"][:, 0, :])
+        quantise_tokens(1, x1_grouped, 1)
+        build_sin_tables(nc.vector, "q", spread["q"][:, 0, :], None)
         build_cos_tables(nc.gpsimd, "k", w_key[:, 0:HEAD])
         build_sin_tables(nc.gpsimd, "k", w_key[:, 0:HEAD], w_key[:, HEAD : HEAD + HALF])
         for first in range(len(banks) + ADD_BEHIND):
@@ -313,12 +316,11 @@ def tile_qwen3nextattentionforengine_pa_kernel(
             if first < len(banks):
                 for m in (2, 3):
                     if first_bank[m] == first + PREPARE_AHEAD:
-                        grouped[m] = flip_tokens(m)
+                        grouped[m] = flip_tokens(m, psum_x, "x")
                     if first_bank[m] == first + QUANTISE_AHEAD:
                         quantise_tokens(m, grouped[m], 1)
                 acc[first] = project(banks[first][0], banks[first][1])
-                sum_sq[first] = sum_squares(acc[first])
-                rstd[first] = inverse_rms(sum_sq[first])
+                rstd[first] = inverse_rms(acc[first], 2 if first < EAGER_BANKS or first == len(banks) - 1 else HEADS_PER_BANK)
             if 0 <= middle < len(banks):
                 pieces[middle] = rotate(banks[middle][0], banks[middle][1], acc[middle], rstd[middle])
             if 0 <= last:

@@ -32,7 +32,7 @@ ADD_BEHIND = 3
 PREPARE_AHEAD = 3
 QUANTISE_AHEAD = 1
 WARM_BEFORE = 3
-WARM_BETWEEN = 1
+WARM_BETWEEN = 3
 EAGER_BANKS = 4
 VECTOR_ADDS = 2
 
@@ -111,10 +111,7 @@ def tile_qwen3nextattentionforengine_pa_kernel(
         cos_sb = keep.tile([P, TOKEN_TILES, HEAD], BF16, name="cos_sb")
         sin_sb = keep.tile([P, TOKEN_TILES, HEAD], BF16, name="sin_sb")
         ones = keep.tile([P, P], BF16, name="ones")
-        gain_rows = {}
-        for kind in ("q", "k"):
-            gain_rows[kind] = keep.tile([P, HEAD], BF16, name="gain_rows_" + kind)
-        w_key = keep.tile([P, HEAD + HALF], F32, name="w_key")
+        gain_rows = keep.tile([P, 2, HEAD], BF16, name="gain_rows")
         ident = keep.tile([P, P], F32, name="ident")
         eps = keep.tile([P, 1], F32, name="eps")
         warm = keep.tile([P, 1], F32, name="warm")
@@ -131,36 +128,17 @@ def tile_qwen3nextattentionforengine_pa_kernel(
         ]
         squares = keep.tile([P, HEADS_PER_BANK, HEAD], F32, name="squares")
 
-        def build_cos_tables(engine, kind, w):
+        def build_tables(kind, w):
             shape = [P, TOKEN_TILES, HALF]
             low = w[:, 0:HALF].unsqueeze(1).to_broadcast(shape)
             high = w[:, HALF:HEAD].unsqueeze(1).to_broadcast(shape)
-            engine.tensor_tensor(out=factors[kind][:, :, 0, 0:HALF], in0=cos_sb[:, :, 0:HALF], in1=low, op=ALU.mult)
-            engine.tensor_tensor(
-                out=factors[kind][:, :, 1, HALF:HEAD], in0=cos_sb[:, :, HALF:HEAD], in1=high, op=ALU.mult
+            table = factors[kind]
+            nc.vector.tensor_tensor(out=table[:, :, 0, 0:HALF], in0=cos_sb[:, :, 0:HALF], in1=low, op=ALU.mult)
+            nc.vector.tensor_tensor(out=table[:, :, 1, HALF:HEAD], in0=cos_sb[:, :, HALF:HEAD], in1=high, op=ALU.mult)
+            nc.vector.tensor_tensor(out=table[:, :, 1, 0:HALF], in0=sin_sb[:, :, HALF:HEAD], in1=low, op=ALU.mult)
+            nc.vector.scalar_tensor_tensor(
+                out=table[:, :, 0, HALF:HEAD], in0=sin_sb[:, :, 0:HALF], scalar=-1.0, in1=high, op0=ALU.mult, op1=ALU.mult
             )
-
-        def build_sin_tables(engine, kind, w, minus_w_high):
-            shape = [P, TOKEN_TILES, HALF]
-            low = w[:, 0:HALF].unsqueeze(1).to_broadcast(shape)
-            high = w[:, HALF:HEAD].unsqueeze(1).to_broadcast(shape)
-            engine.tensor_tensor(out=factors[kind][:, :, 1, 0:HALF], in0=sin_sb[:, :, HALF:HEAD], in1=low, op=ALU.mult)
-            if minus_w_high is None:
-                engine.scalar_tensor_tensor(
-                    out=factors[kind][:, :, 0, HALF:HEAD],
-                    in0=sin_sb[:, :, 0:HALF],
-                    scalar=-1.0,
-                    in1=high,
-                    op0=ALU.mult,
-                    op1=ALU.mult,
-                )
-            else:
-                engine.tensor_tensor(
-                    out=factors[kind][:, :, 0, HALF:HEAD],
-                    in0=sin_sb[:, :, 0:HALF],
-                    in1=minus_w_high.unsqueeze(1).to_broadcast(shape),
-                    op=ALU.mult,
-                )
 
         def flip_tokens(m, pool, tag):
             words = x_sb[m][:].bitcast(F32)
@@ -251,9 +229,8 @@ def tile_qwen3nextattentionforengine_pa_kernel(
 
         ctx.enter_context(tc.manual_schedule())
 
-        nc.vector.memset(gain_rows["q"][:], 0.0)
+        nc.vector.memset(gain_rows[:], 0.0)
         nc.vector.memset(ones[:], 1.0)
-        nc.vector.memset(gain_rows["k"][:], 0.0)
         nc.vector.memset(w_scales[0][:].bitcast(I32), 0)
         nc.vector.memset(eps[:], EPS)
         for c in range(1, len(chunks)):
@@ -272,13 +249,13 @@ def tile_qwen3nextattentionforengine_pa_kernel(
                 )
 
         load_x(0, 1)
-        nc.sync.dma_start(out=gain_rows["q"][0:1, :], in_=q_norm_w.unsqueeze(0))
-        nc.gpsimd.dma_start(out=gain_rows["k"][0:1, :], in_=k_norm_w.unsqueeze(0))
+        nc.scalar.dma_start(out=cos_sb[:], in_=cos_tiles)
+        nc.scalar.dma_start(out=sin_sb[:], in_=sin_tiles)
+        nc.sync.dma_start(out=gain_rows[0:1, 0, :], in_=q_norm_w.unsqueeze(0))
+        nc.sync.dma_start(out=gain_rows[0:1, 1, :], in_=k_norm_w.unsqueeze(0))
         load_x(1, 1)
         load_words(0)
         load_scales(0)
-        nc.sync.dma_start(out=cos_sb[:], in_=cos_tiles)
-        nc.sync.dma_start(out=sin_sb[:], in_=sin_tiles)
         for c in range(1, len(chunks)):
             load_words(c)
             load_scales(c)
@@ -296,20 +273,21 @@ def tile_qwen3nextattentionforengine_pa_kernel(
         pieces = {}
 
         idle_matmuls(WARM_BEFORE)
-        quantise_tokens(0, flip_tokens(0, psum_x, "x"), 2)
+        spread = psum_acc.tile([P, HEADS_PER_BANK, HEAD], F32, name="spread", tag="acc")
+        nc.tensor.matmul(
+            out=spread[:, 0:2, :].rearrange("p w d -> p (w d)"),
+            lhsT=ones[:],
+            rhs=gain_rows[:].rearrange("p w d -> p (w d)"),
+            start=True,
+            stop=True,
+        )
+        x0_grouped = flip_tokens(0, psum_x, "x")
         x1_grouped = flip_tokens(1, psum_acc, "acc")
-        spread = {}
-        for kind in ("q", "k"):
-            spread[kind] = psum_acc.tile([P, HEADS_PER_BANK, HEAD], F32, name="spread", tag="acc")
-            nc.tensor.matmul(out=spread[kind][:, 0, :], lhsT=ones[:], rhs=gain_rows[kind][:], start=True, stop=True)
         idle_matmuls(WARM_BETWEEN)
-        nc.scalar.copy(out=w_key[:, 0:HEAD], in_=spread["k"][:, 0, :])
-        nc.scalar.activation(out=w_key[:, HEAD : HEAD + HALF], in_=spread["k"][:, 0, HALF:HEAD], func=ACT.Copy, scale=-1.0)
-        build_cos_tables(nc.vector, "q", spread["q"][:, 0, :])
+        build_tables("q", spread[:, 0, :])
+        quantise_tokens(0, x0_grouped, 2)
         quantise_tokens(1, x1_grouped, 1)
-        build_sin_tables(nc.vector, "q", spread["q"][:, 0, :], None)
-        build_cos_tables(nc.gpsimd, "k", w_key[:, 0:HEAD])
-        build_sin_tables(nc.gpsimd, "k", w_key[:, 0:HEAD], w_key[:, HEAD : HEAD + HALF])
+        build_tables("k", spread[:, 1, :])
         for first in range(len(banks) + ADD_BEHIND):
             middle = first - ROTATE_BEHIND
             last = first - ADD_BEHIND

@@ -204,28 +204,33 @@ def tile_qwen3nextattentionforengine_pa_kernel(
                 )
             return rstd
 
-        def rotate(m, c, acc, rstd):
+        def rotate(m, c, acc, rstd, pieces, place):
             kind = chunks[c][0]
-            pieces = products.tile([P, 2 * HEADS_PER_BANK, 2, HALF], F32, name="pieces")
+            row = 2 * HEADS_PER_BANK * place
             for h in range(HEADS_PER_BANK):
                 nc.vector.scalar_tensor_tensor(
-                    out=pieces[:, 2 * h : 2 * h + 2, :, :].rearrange("p x s j -> p x (s j)"),
+                    out=pieces[:, row + 2 * h : row + 2 * h + 2, :, :].rearrange("p x s j -> p x (s j)"),
                     in0=acc[:, h, :].unsqueeze(1).to_broadcast([P, 2, HEAD]),
                     scalar=rstd[:, h : h + 1],
                     in1=factors[kind][:, m, :, :],
                     op0=ALU.mult,
                     op1=ALU.mult,
                 )
-            return pieces
 
-        def add_and_store(adder, m, c, pieces):
-            n, tiles = chunks[c][3], chunks[c][4]
-            rotated = results.tile([P, 2 * HEADS_PER_BANK, HALF], F32, name="rotated")
-            adder.tensor_tensor(out=rotated[:], in0=pieces[:, :, 0, :], in1=pieces[:, :, 1, :], op=ALU.add)
-            nc.sync.dma_start(
-                out=tiles[m][:, n * N_TILE : (n + 1) * N_TILE],
-                in_=rotated[:].rearrange("p x j -> p (x j)"),
+        def add_and_store(adder, members, pieces):
+            rows = 2 * HEADS_PER_BANK
+            used = rows * len(members)
+            rotated = results.tile([P, 2 * rows, HALF], F32, name="rotated")
+            adder.tensor_tensor(
+                out=rotated[:, 0:used, :], in0=pieces[:, 0:used, 0, :], in1=pieces[:, 0:used, 1, :], op=ALU.add
             )
+            for place in range(len(members)):
+                m, c = banks[members[place]]
+                n, tiles = chunks[c][3], chunks[c][4]
+                nc.sync.dma_start(
+                    out=tiles[m][:, n * N_TILE : (n + 1) * N_TILE],
+                    in_=rotated[:, place * rows : (place + 1) * rows, :].rearrange("p x j -> p (x j)"),
+                )
 
         ctx.enter_context(tc.manual_schedule())
 
@@ -271,6 +276,8 @@ def tile_qwen3nextattentionforengine_pa_kernel(
         acc = {}
         rstd = {}
         pieces = {}
+        groups = [[0], [1, 2], [3, 4], [5, 6], [7], [8, 9], [10, 11], [12, 13], [14, 15], [16], [17], [18], [19]]
+        group_of = dict([(g[i], (n, i)) for n, g in enumerate(groups) for i in range(len(g))])
 
         idle_matmuls(WARM_BEFORE)
         spread = psum_acc.tile([P, HEADS_PER_BANK, HEAD], F32, name="spread", tag="acc")
@@ -300,7 +307,12 @@ def tile_qwen3nextattentionforengine_pa_kernel(
                 acc[first] = project(banks[first][0], banks[first][1])
                 rstd[first] = inverse_rms(acc[first], 2 if first < EAGER_BANKS or first == len(banks) - 1 else HEADS_PER_BANK)
             if 0 <= middle < len(banks):
-                pieces[middle] = rotate(banks[middle][0], banks[middle][1], acc[middle], rstd[middle])
+                group, place = group_of[middle]
+                if place == 0:
+                    pieces[group] = products.tile([P, 4 * HEADS_PER_BANK, 2, HALF], F32, name="pieces")
+                rotate(banks[middle][0], banks[middle][1], acc[middle], rstd[middle], pieces[group], place)
             if 0 <= last:
-                adder = nc.vector if last >= len(banks) - VECTOR_ADDS else nc.gpsimd
-                add_and_store(adder, banks[last][0], banks[last][1], pieces[last])
+                group, place = group_of[last]
+                if place == len(groups[group]) - 1:
+                    adder = nc.vector if last >= len(banks) - VECTOR_ADDS else nc.gpsimd
+                    add_and_store(adder, groups[group], pieces[group])

@@ -76,11 +76,11 @@ def tile_qwen3nextattentionforengine_pa_kernel(
         for n in range(K_FEATURES // N_TILE):
             chunks.append(("k", Wk_words, Wk_scales, n, k_tiles))
         w_words = [
-            keep.tile([P, PASSES, 2 * N_TILE], U8, name="w_words%d" % c, align_bytes=64)
+            keep.tile([P, PASSES, 2 * N_TILE], U8, name="w_words%d" % c, align_bytes=256)
             for c in range(len(chunks))
         ]
         w_scales = [
-            keep.tile([P, PASSES, N_TILE], U8, name="w_scales%d" % c, align_bytes=64)
+            keep.tile([P, PASSES, N_TILE], U8, name="w_scales%d" % c, align_bytes=256)
             for c in range(len(chunks))
         ]
 
@@ -119,11 +119,11 @@ def tile_qwen3nextattentionforengine_pa_kernel(
         for kind in ("q", "k"):
             factors[kind] = keep.tile([P, TOKEN_TILES, 2, HEAD], F32, name="factors_" + kind)
         x_codes = [
-            keep.tile([P, PASSES * P], U32, name="x_codes%d" % m, align_bytes=64)
+            keep.tile([P, PASSES * P], U32, name="x_codes%d" % m, align_bytes=256)
             for m in range(TOKEN_TILES)
         ]
         x_scales = [
-            keep.tile([P, PASSES * P], U8, name="x_scales%d" % m, align_bytes=64)
+            keep.tile([P, PASSES * P], U8, name="x_scales%d" % m, align_bytes=256)
             for m in range(TOKEN_TILES)
         ]
         squares = keep.tile([P, HEADS_PER_BANK, HEAD], F32, name="squares")
@@ -142,7 +142,7 @@ def tile_qwen3nextattentionforengine_pa_kernel(
 
         def flip_tokens(m, pool, tag):
             words = x_sb[m][:].bitcast(F32)
-            grouped = stage.tile([P, PASSES * P * 4], BF16, name="grouped", align_bytes=64)
+            grouped = stage.tile([P, PASSES * P * 4], BF16, name="grouped", align_bytes=256)
             grouped_words = grouped[:].bitcast(F32).rearrange("p (g t u) -> p g t u", g=PASSES, u=2)
             flipped = []
             for pair in range(PASSES // 2):

@@ -33,7 +33,6 @@ PREPARE_AHEAD = 3
 QUANTISE_AHEAD = 1
 WARM_BEFORE = 3
 WARM_BETWEEN = 3
-EAGER_BANKS = 4
 VECTOR_ADDS = 2
 
 FLOPS = 2 * TOKENS * HID * FEATURES
@@ -305,7 +304,7 @@ def tile_qwen3nextattentionforengine_pa_kernel(
                     if first_bank[m] == first + QUANTISE_AHEAD:
                         quantise_tokens(m, grouped[m], 1)
                 acc[first] = project(banks[first][0], banks[first][1])
-                rstd[first] = inverse_rms(acc[first], 2 if first < EAGER_BANKS or first == len(banks) - 1 else HEADS_PER_BANK)
+                rstd[first] = inverse_rms(acc[first], 2 if first == len(banks) - 1 else HEADS_PER_BANK)
             if 0 <= middle < len(banks):
                 group, place = group_of[middle]
                 if place == 0:

@@ -62,13 +62,13 @@ def tile_qwen3nextattentionforengine_pa_kernel(
     with ExitStack() as ctx:
         keep = ctx.enter_context(tc.tile_pool(name="keep", bufs=1))
         stage = ctx.enter_context(tc.tile_pool(name="stage", bufs=2))
-        small = ctx.enter_context(tc.tile_pool(name="small", bufs=8))
+        small = ctx.enter_context(tc.tile_pool(name="small", bufs=24))
         products = ctx.enter_context(tc.tile_pool(name="products", bufs=4))
         results = ctx.enter_context(tc.tile_pool(name="results", bufs=6))
         psum_x = ctx.enter_context(tc.psum_pool(name="psum_x", bufs=2))
         psum_acc = ctx.enter_context(tc.psum_pool(name="psum_acc", bufs=6))
 
-        x_sb = [keep.tile([P, HID], BF16, name="x_sb%d" % m) for m in range(TOKEN_TILES)]
+        x_sb = [keep.tile([P, HID], BF16, name="x_sb%d" % m, align_bytes=256) for m in range(TOKEN_TILES)]
         chunks = []
         for n in range(Q_FEATURES // N_TILE):
             chunks.append(("q", Wq_query_words, Wq_query_scales, n, q_tiles))
@@ -107,16 +107,16 @@ def tile_qwen3nextattentionforengine_pa_kernel(
                     in_=by_row[r][:, :, n * width : (n + 1) * width],
                 )
 
-        cos_sb = keep.tile([P, TOKEN_TILES, HEAD], BF16, name="cos_sb")
-        sin_sb = keep.tile([P, TOKEN_TILES, HEAD], BF16, name="sin_sb")
+        cos_sb = keep.tile([P, TOKEN_TILES, HEAD], BF16, name="cos_sb", align_bytes=256)
+        sin_sb = keep.tile([P, TOKEN_TILES, HEAD], BF16, name="sin_sb", align_bytes=256)
         ones = keep.tile([P, P], BF16, name="ones")
         gain_rows = keep.tile([P, 2, HEAD], BF16, name="gain_rows")
-        ident = keep.tile([P, P], F32, name="ident")
+        ident = keep.tile([P, P], F32, name="ident", align_bytes=256)
         eps = keep.tile([P, 1], F32, name="eps")
         warm = keep.tile([P, 1], F32, name="warm")
         factors = {}
         for kind in ("q", "k"):
-            factors[kind] = keep.tile([P, TOKEN_TILES, 2, HEAD], F32, name="factors_" + kind)
+            factors[kind] = keep.tile([P, TOKEN_TILES, 2, HEAD], F32, name="factors_" + kind, align_bytes=256)
         x_codes = [
             keep.tile([P, PASSES * P], U32, name="x_codes%d" % m, align_bytes=256)
             for m in range(TOKEN_TILES)
@@ -125,7 +125,6 @@ def tile_qwen3nextattentionforengine_pa_kernel(
             keep.tile([P, PASSES * P], U8, name="x_scales%d" % m, align_bytes=256)
             for m in range(TOKEN_TILES)
         ]
-        squares = keep.tile([P, HEADS_PER_BANK, HEAD], F32, name="squares")
 
         def build_tables(kind, w):
             shape = [P, TOKEN_TILES, HALF]
@@ -185,14 +184,14 @@ def tile_qwen3nextattentionforengine_pa_kernel(
                 )
             return acc
 
-        def inverse_rms(acc, group):
+        def inverse_rms(bank, acc, group):
             sum_sq = small.tile([P, HEADS_PER_BANK], F32, name="sum_sq")
             rstd = small.tile([P, HEADS_PER_BANK], F32, name="rstd")
             for begin in range(0, HEADS_PER_BANK, group):
                 end = begin + group
                 for h in range(begin, end):
                     nc.scalar.activation(
-                        out=squares[:, h, :], in_=acc[:, h, :], func=ACT.Square, accum_out=sum_sq[:, h : h + 1]
+                        out=squares[:, bank, h, :], in_=acc[:, h, :], func=ACT.Square, accum_out=sum_sq[:, h : h + 1]
                     )
                 nc.scalar.activation(
                     out=rstd[:, begin:end],
@@ -219,7 +218,7 @@ def tile_qwen3nextattentionforengine_pa_kernel(
         def add_and_store(adder, members, pieces):
             rows = 2 * HEADS_PER_BANK
             used = rows * len(members)
-            rotated = results.tile([P, 2 * rows, HALF], F32, name="rotated")
+            rotated = results.tile([P, 2 * rows, HALF], F32, name="rotated", align_bytes=256)
             adder.tensor_tensor(
                 out=rotated[:, 0:used, :], in0=pieces[:, 0:used, 0, :], in1=pieces[:, 0:used, 1, :], op=ALU.add
             )
@@ -270,6 +269,7 @@ def tile_qwen3nextattentionforengine_pa_kernel(
 
         banks = [(m, c) for c in range(len(chunks)) for m in (0, 1)]
         banks.extend([(m, c) for m in (2, 3) for c in range(len(chunks))])
+        squares = keep.tile([P, len(banks), HEADS_PER_BANK, HEAD], BF16, name="squares", align_bytes=256)
         first_bank = dict([(m, min([i for i in range(len(banks)) if banks[i][0] == m])) for m in range(TOKEN_TILES)])
         grouped = {}
         acc = {}
@@ -304,11 +304,11 @@ def tile_qwen3nextattentionforengine_pa_kernel(
                     if first_bank[m] == first + QUANTISE_AHEAD:
                         quantise_tokens(m, grouped[m], 1)
                 acc[first] = project(banks[first][0], banks[first][1])
-                rstd[first] = inverse_rms(acc[first], 2 if first == len(banks) - 1 else HEADS_PER_BANK)
+                rstd[first] = inverse_rms(first, acc[first], HEADS_PER_BANK)
             if 0 <= middle < len(banks):
                 group, place = group_of[middle]
                 if place == 0:
-                    pieces[group] = products.tile([P, 4 * HEADS_PER_BANK, 2, HALF], F32, name="pieces")
+                    pieces[group] = products.tile([P, 4 * HEADS_PER_BANK, 2, HALF], F32, name="pieces", align_bytes=256)
                 rotate(banks[middle][0], banks[middle][1], acc[middle], rstd[middle], pieces[group], place)
             if 0 <= last:
                 group, place = group_of[last]

from contextlib import ExitStack

import concourse.mybir as mybir
from concourse.masks import make_identity

F32 = mybir.dt.float32
BF16 = mybir.dt.bfloat16
I32 = mybir.dt.int32
U32 = mybir.dt.uint32
U8 = mybir.dt.uint8
FP8X4 = mybir.dt.float8_e4m3fn_x4
FP4X4 = mybir.dt.float4_e2m1fn_x4
ALU = mybir.AluOpType
ACT = mybir.ActivationFunctionType

P = 128
TOKENS = 512
TOKEN_TILES = TOKENS // P
HID = 2048
K_PASS = 512
PASSES = HID // K_PASS
HEAD = 128
HALF = HEAD // 2
N_TILE = 512
HEADS_PER_BANK = N_TILE // HEAD
Q_FEATURES = 2048
K_FEATURES = 512
FEATURES = Q_FEATURES + K_FEATURES
EPS = 1e-6
ROTATE_BEHIND = 2
ADD_BEHIND = 3
PREPARE_AHEAD = 3
QUANTISE_AHEAD = 1
WARM_BEFORE = 3
WARM_BETWEEN = 3
VECTOR_ADDS = 2

FLOPS = 2 * TOKENS * HID * FEATURES


def tile_qwen3nextattentionforengine_pa_kernel(
    tc,
    hidden_states,
    cos,
    sin,
    Wq_query_words,
    Wq_query_scales,
    Wk_words,
    Wk_scales,
    q_norm_w,
    k_norm_w,
    out_0,
    out_1,
):
    nc = tc.nc
    x_tiles = hidden_states.rearrange("b s k -> (b s) k").rearrange("(p m) k -> m p k", m=TOKEN_TILES)
    q_tiles = out_0.rearrange("b s h d -> (b s) (h d)").rearrange("(p m) f -> m p f", m=TOKEN_TILES)
    k_tiles = out_1.rearrange("b s h d -> (b s) (h d)").rearrange("(p m) f -> m p f", m=TOKEN_TILES)
    cos_tiles = cos.rearrange("b s d -> (b s) d").rearrange("(p m) d -> p m d", m=TOKEN_TILES)
    sin_tiles = sin.rearrange("b s d -> (b s) d").rearrange("(p m) d -> p m d", m=TOKEN_TILES)

    with ExitStack() as ctx:
        keep = ctx.enter_context(tc.tile_pool(name="keep", bufs=1))
        stage = ctx.enter_context(tc.tile_pool(name="stage", bufs=2))
        small = ctx.enter_context(tc.tile_pool(name="small", bufs=24))
        products = ctx.enter_context(tc.tile_pool(name="products", bufs=4))
        results = ctx.enter_context(tc.tile_pool(name="results", bufs=6))
        psum_x = ctx.enter_context(tc.psum_pool(name="psum_x", bufs=2))
        psum_acc = ctx.enter_context(tc.psum_pool(name="psum_acc", bufs=6))

        x_sb = [keep.tile([P, HID], BF16, name="x_sb%d" % m, align_bytes=256) for m in range(TOKEN_TILES)]
        chunks = []
        for n in range(Q_FEATURES // N_TILE):
            chunks.append(("q", Wq_query_words, Wq_query_scales, n, q_tiles))
        for n in range(K_FEATURES // N_TILE):
            chunks.append(("k", Wk_words, Wk_scales, n, k_tiles))
        w_words = [
            keep.tile([P, PASSES, 2 * N_TILE], U8, name="w_words%d" % c, align_bytes=256)
            for c in range(len(chunks))
        ]
        w_scales = [
            keep.tile([P, PASSES, N_TILE], U8, name="w_scales%d" % c, align_bytes=256)
            for c in range(len(chunks))
        ]

        def load_x(m, parts):
            width = HID // parts
            for begin in range(0, HID, width):
                nc.sync.dma_start(out=x_sb[m][:, begin : begin + width], in_=x_tiles[m][:, begin : begin + width])

        def load_words(c):
            words, n = chunks[c][1], chunks[c][3]
            by_partition = words.bitcast(I32).rearrange("g p w -> p g w")
            width = 2 * N_TILE // 4
            nc.sync.dma_start(
                out=w_words[c][:].bitcast(I32),
                in_=by_partition[:, :, n * width : (n + 1) * width],
            )

        def load_scales(c):
            scales, n = chunks[c][2], chunks[c][3]
            by_row = scales.bitcast(I32).rearrange("g (Q r) w -> r Q g w", r=4)
            width = N_TILE // 4
            for r in range(4):
                nc.sync.dma_start(
                    out=w_scales[c][r:P:32, :, :].bitcast(I32),
                    in_=by_row[r][:, :, n * width : (n + 1) * width],
                )

        cos_sb = keep.tile([P, TOKEN_TILES, HEAD], BF16, name="cos_sb", align_bytes=256)
        sin_sb = keep.tile([P, TOKEN_TILES, HEAD], BF16, name="sin_sb", align_bytes=256)
        ones = keep.tile([P, P], BF16, name="ones")
        gain_rows = keep.tile([P, 2, HEAD], BF16, name="gain_rows")
        ident = keep.tile([P, P], F32, name="ident", align_bytes=256)
        eps = keep.tile([P, 1], F32, name="eps")
        warm = keep.tile([P, 1], F32, name="warm")
        factors = {}
        for kind in ("q", "k"):
            factors[kind] = keep.tile([P, TOKEN_TILES, 2, HEAD], F32, name="factors_" + kind, align_bytes=256)
        x_codes = [
            keep.tile([P, PASSES * P], U32, name="x_codes%d" % m, align_bytes=256)
            for m in range(TOKEN_TILES)
        ]
        x_scales = [
            keep.tile([P, PASSES * P], U8, name="x_scales%d" % m, align_bytes=256)
            for m in range(TOKEN_TILES)
        ]

        def build_tables(kind, w):
            shape = [P, TOKEN_TILES, HALF]
            low = w[:, 0:HALF].unsqueeze(1).to_broadcast(shape)
            high = w[:, HALF:HEAD].unsqueeze(1).to_broadcast(shape)
            table = factors[kind]
            nc.vector.tensor_tensor(out=table[:, :, 0, 0:HALF], in0=cos_sb[:, :, 0:HALF], in1=low, op=ALU.mult)
            nc.vector.tensor_tensor(out=table[:, :, 1, HALF:HEAD], in0=cos_sb[:, :, HALF:HEAD], in1=high, op=ALU.mult)
            nc.vector.tensor_tensor(out=table[:, :, 1, 0:HALF], in0=sin_sb[:, :, HALF:HEAD], in1=low, op=ALU.mult)
            nc.vector.scalar_tensor_tensor(
                out=table[:, :, 0, HALF:HEAD], in0=sin_sb[:, :, 0:HALF], scalar=-1.0, in1=high, op0=ALU.mult, op1=ALU.mult
            )

        def flip_tokens(m, pool, tag):
            words = x_sb[m][:].bitcast(F32)
            grouped = stage.tile([P, PASSES * P * 4], BF16, name="grouped", align_bytes=256)
            grouped_words = grouped[:].bitcast(F32).rearrange("p (g t u) -> p g t u", g=PASSES, u=2)
            flipped = []
            for pair in range(PASSES // 2):
                flipped.append(pool.tile([P, 2, 2, P], F32, name="flipped", tag=tag))
                for i in range(2):
                    g = 2 * pair + i
                    for u in range(2):
                        nc.tensor.transpose(
                            flipped[pair][:, i, u, :],
                            words[:, 256 * g + u : 256 * (g + 1) : 2],
                            ident[:],
                        )
            for pair in range(PASSES // 2):
                nc.scalar.copy(
                    out=grouped_words[:, 2 * pair : 2 * pair + 2, :, :],
                    in_=flipped[pair][:].rearrange("p i u t -> p i t u"),
                )
            return grouped

        def quantise_tokens(m, grouped, calls):
            width = PASSES * P // calls
            for begin in range(0, PASSES * P, width):
                end = begin + width
                nc.vector.quantize_mx(
                    out=x_codes[m][:, begin:end].bitcast(FP8X4),
                    scales=x_scales[m][:, begin:end],
                    in_=grouped[:, 4 * begin : 4 * end],
                )

        def project(m, c):
            acc = psum_acc.tile([P, HEADS_PER_BANK, HEAD], F32, name="acc")
            for g in range(PASSES):
                nc.tensor.matmul_mx(
                    out=acc[:].rearrange("p h d -> p (h d)"),
                    lhsT=x_codes[m][:, g * P : (g + 1) * P].bitcast(FP8X4),
                    lhsT_scale=x_scales[m][:, g * P : (g + 1) * P],
                    rhs=w_words[c][:, g, :].bitcast(FP4X4),
                    rhs_scale=w_scales[c][:, g, :],
                    start=(g == 0),
                    stop=(g == PASSES - 1),
                )
            return acc

        def inverse_rms(bank, acc, group):
            sum_sq = small.tile([P, HEADS_PER_BANK], F32, name="sum_sq")
            rstd = small.tile([P, HEADS_PER_BANK], F32, name="rstd")
            for begin in range(0, HEADS_PER_BANK, group):
                end = begin + group
                for h in range(begin, end):
                    nc.scalar.activation(
                        out=squares[:, bank, h, :], in_=acc[:, h, :], func=ACT.Square, accum_out=sum_sq[:, h : h + 1]
                    )
                nc.scalar.activation(
                    out=rstd[:, begin:end],
                    in_=sum_sq[:, begin:end],
                    func=ACT.Abs_reciprocal_sqrt,
                    scale=1.0 / HEAD,
                    bias=eps[:, 0:1],
                )
            return rstd

        def rotate(m, c, acc, rstd, pieces, place):
            kind = chunks[c][0]
            row = 2 * HEADS_PER_BANK * place
            for h in range(HEADS_PER_BANK):
                nc.vector.scalar_tensor_tensor(
                    out=pieces[:, row + 2 * h : row + 2 * h + 2, :, :].rearrange("p x s j -> p x (s j)"),
                    in0=acc[:, h, :].unsqueeze(1).to_broadcast([P, 2, HEAD]),
                    scalar=rstd[:, h : h + 1],
                    in1=factors[kind][:, m, :, :],
                    op0=ALU.mult,
                    op1=ALU.mult,
                )

        def add_and_store(adder, members, pieces):
            rows = 2 * HEADS_PER_BANK
            used = rows * len(members)
            rotated = results.tile([P, 2 * rows, HALF], F32, name="rotated", align_bytes=256)
            adder.tensor_tensor(
                out=rotated[:, 0:used, :], in0=pieces[:, 0:used, 0, :], in1=pieces[:, 0:used, 1, :], op=ALU.add
            )
            for place in range(len(members)):
                m, c = banks[members[place]]
                n, tiles = chunks[c][3], chunks[c][4]
                nc.sync.dma_start(
                    out=tiles[m][:, n * N_TILE : (n + 1) * N_TILE],
                    in_=rotated[:, place * rows : (place + 1) * rows, :].rearrange("p x j -> p (x j)"),
                )

        ctx.enter_context(tc.manual_schedule())

        nc.vector.memset(gain_rows[:], 0.0)
        nc.vector.memset(ones[:], 1.0)
        nc.vector.memset(w_scales[0][:].bitcast(I32), 0)
        nc.vector.memset(eps[:], EPS)
        for c in range(1, len(chunks)):
            nc.vector.memset(w_scales[c][:].bitcast(I32), 0)
        make_identity(nc, ident[:])

        def idle_matmuls(count):
            idle = psum_acc.tile([P, HEADS_PER_BANK, HEAD], F32, name="idle", tag="acc")
            for i in range(count):
                nc.tensor.matmul(
                    out=idle[:],
                    lhsT=ones[:],
                    rhs=ones[:].unsqueeze(1).to_broadcast([P, HEADS_PER_BANK, HEAD]),
                    start=True,
                    stop=True,
                )

        load_x(0, 1)
        nc.scalar.dma_start(out=cos_sb[:], in_=cos_tiles)
        nc.scalar.dma_start(out=sin_sb[:], in_=sin_tiles)
        nc.sync.dma_start(out=gain_rows[0:1, 0, :], in_=q_norm_w.unsqueeze(0))
        nc.sync.dma_start(out=gain_rows[0:1, 1, :], in_=k_norm_w.unsqueeze(0))
        load_x(1, 1)
        load_words(0)
        load_scales(0)
        for c in range(1, len(chunks)):
            load_words(c)
            load_scales(c)
        load_x(2, 2)
        load_x(3, 2)

        nc.scalar.activation(out=warm[:], in_=eps[:], func=ACT.Abs_reciprocal_sqrt)

        banks = [(m, c) for c in range(len(chunks)) for m in (0, 1)]
        banks.extend([(m, c) for m in (2, 3) for c in range(len(chunks))])
        squares = keep.tile([P, len(banks), HEADS_PER_BANK, HEAD], BF16, name="squares", align_bytes=256)
        first_bank = dict([(m, min([i for i in range(len(banks)) if banks[i][0] == m])) for m in range(TOKEN_TILES)])
        grouped = {}
        acc = {}
        rstd = {}
        pieces = {}
        groups = [[0], [1, 2], [3, 4], [5, 6], [7], [8, 9], [10, 11], [12, 13], [14, 15], [16], [17], [18], [19]]
        group_of = dict([(g[i], (n, i)) for n, g in enumerate(groups) for i in range(len(g))])

        idle_matmuls(WARM_BEFORE)
        spread = psum_acc.tile([P, HEADS_PER_BANK, HEAD], F32, name="spread", tag="acc")
        nc.tensor.matmul(
            out=spread[:, 0:2, :].rearrange("p w d -> p (w d)"),
            lhsT=ones[:],
            rhs=gain_rows[:].rearrange("p w d -> p (w d)"),
            start=True,
            stop=True,
        )
        x0_grouped = flip_tokens(0, psum_x, "x")
        x1_grouped = flip_tokens(1, psum_acc, "acc")
        idle_matmuls(WARM_BETWEEN)
        build_tables("q", spread[:, 0, :])
        quantise_tokens(0, x0_grouped, 2)
        quantise_tokens(1, x1_grouped, 1)
        build_tables("k", spread[:, 1, :])
        for first in range(len(banks) + ADD_BEHIND):
            middle = first - ROTATE_BEHIND
            last = first - ADD_BEHIND
            if first < len(banks):
                for m in (2, 3):
                    if first_bank[m] == first + PREPARE_AHEAD:
                        grouped[m] = flip_tokens(m, psum_x, "x")
                    if first_bank[m] == first + QUANTISE_AHEAD:
                        quantise_tokens(m, grouped[m], 1)
                acc[first] = project(banks[first][0], banks[first][1])
                rstd[first] = inverse_rms(first, acc[first], HEADS_PER_BANK)
            if 0 <= middle < len(banks):
                group, place = group_of[middle]
                if place == 0:
                    pieces[group] = products.tile([P, 4 * HEADS_PER_BANK, 2, HALF], F32, name="pieces", align_bytes=256)
                rotate(banks[middle][0], banks[middle][1], acc[middle], rstd[middle], pieces[group], place)
            if 0 <= last:
                group, place = group_of[last]
                if place == len(groups[group]) - 1:
                    adder = nc.vector if last >= len(banks) - VECTOR_ADDS else nc.gpsimd
                    add_and_store(adder, groups[group], pieces[group])
